import numpy as np
import ml_dtypes


def mxq(x, axis, fmt="e4m3"):
    dtype, down = {"e4m3": (ml_dtypes.float8_e4m3fn, 7), "e5m2": (ml_dtypes.float8_e5m2, 14)}[fmt]
    v = np.moveaxis(np.asarray(x, np.float32).astype(ml_dtypes.bfloat16).astype(np.float64), axis, -1)
    blocks = v.reshape(v.shape[:-1] + (-1, 32))
    amax = np.abs(blocks).max(-1, keepdims=True)
    byte = np.maximum(np.where(amax > 0, np.frexp(amax)[1] - 1 + 127, 0) - down, 1)
    scale = np.exp2(byte - 127.0)
    codes = (blocks / scale).astype(np.float32).astype(dtype).astype(np.float64)
    return np.moveaxis((codes * scale).reshape(v.shape), -1, axis)


WIDE = False


def mx_kscale(k):
    if not WIDE:
        return np.ones(k)
    levels = np.array([10, -10, 5, -5, 0])
    a = np.random.permutation(np.resize(levels, k // 512 * 4)).reshape(k // 512, 4)
    idx = np.arange(k)
    return np.exp2(a[idx // 512, idx % 128 // 32])


BF16 = ml_dtypes.bfloat16


def bf(x):
    return np.asarray(x, np.float32).astype(BF16)


def f64(x):
    return np.asarray(x).astype(np.float64)


E2M1 = np.array([0.0, 0.5, 1.0, 1.5, 2.0, 3.0, 4.0, 6.0, -0.0, -0.5, -1.0, -1.5, -2.0, -3.0, -4.0, -6.0])


def pack_weight(w, fmt):
    k, n = w.shape
    w = f64(bf(w)).reshape(k // 32, 32, n)
    amax = np.abs(w).max(1)
    if fmt == "e4m3":
        byte = np.frexp(amax)[1] - 1 + 127 - 7
    else:
        mant, ex = np.frexp(amax / 6.0)
        byte = np.where(mant > 0.5, ex, ex - 1) + 127
    byte = np.clip(np.where(amax > 0, byte, 1), 1, 254)
    scaled = (w * np.exp2(127.0 - byte)[:, None, :]).reshape(k, n).astype(np.float32)
    by_word = np.ascontiguousarray(scaled.reshape(k // 512, 128, 4, n).transpose(0, 1, 3, 2))
    if fmt == "e4m3":
        words = by_word.astype(ml_dtypes.float8_e4m3fn).view(np.uint8)
    else:
        c = by_word.astype(ml_dtypes.float4_e2m1fn).view(np.uint8) & 0xF
        words = c[..., 0::2] | (c[..., 1::2] << 4)
    return np.ascontiguousarray(words), np.ascontiguousarray(byte.astype(np.uint8).reshape(k // 512, 16, n))


def unpack_weight(words, scales, fmt):
    g, p, n, _ = words.shape
    if fmt == "e4m3":
        vals = np.ascontiguousarray(words).view(ml_dtypes.float8_e4m3fn).astype(np.float64)
    else:
        nib = np.empty((g, p, n, 4), np.uint8)
        nib[..., 0::2] = words & 0xF
        nib[..., 1::2] = words >> 4
        vals = E2M1[nib]
    vals = vals * np.repeat(np.exp2(scales.astype(np.float64) - 127.0), 8, axis=1)[..., None]
    return vals.transpose(0, 1, 3, 2).reshape(g * 512, n)


B, I, P, F = 256, 8192, 256, 1024
FMT = "e4m3"


def setup_inputs():
    s = mx_kscale(I)
    x = bf(np.random.standard_normal((B, I)) * s)
    features_words, features_scales = pack_weight((np.random.uniform(-1.0, 1.0, (F, I)) * np.sqrt(3.0 / I) / s).T, FMT)
    prototypes_words, prototypes_scales = pack_weight((np.random.uniform(-1.0, 1.0, (P, I)) * np.sqrt(3.0) * s).T, FMT)
    return {"x": x,
            "features_words": features_words,
            "features_scales": features_scales,
            "prototypes_words": prototypes_words,
            "prototypes_scales": prototypes_scales,
            "alpha": bf((2.0 + 0.3 * np.random.standard_normal(1)) / F),
            "beta": bf((1.5 + 0.3 * np.random.standard_normal(1)) / F),
            "theta": bf((8.0 + np.random.standard_normal(1)) / F)}


def reference(x, features_words, features_scales, prototypes_words, prototypes_scales, alpha, beta, theta):
    fq = unpack_weight(features_words, features_scales, FMT).T
    pq = unpack_weight(prototypes_words, prototypes_scales, FMT).T
    xf = mxq(f64(x), 1, "e4m3") @ fq.T
    pf = pq @ fq.T
    x_pres = np.maximum(xf, 0.0)
    p_pres = np.maximum(pf, 0.0)
    a = xf * x_pres
    c = pf * p_pres
    aq = mxq(a, 1, "e4m3")
    cq = mxq(c, 1, "e4m3")
    common = aq @ cq.T
    x_distinctive = aq @ mxq(1.0 - p_pres, 1, "e4m3").T
    p_distinctive = mxq(1.0 - x_pres, 1, "e4m3") @ cq.T
    return f64(theta) * common - f64(alpha) * x_distinctive - f64(beta) * p_distinctive

@@ -1,0 +1,280 @@
+from contextlib import ExitStack
+
+import concourse.mybir as mybir
+from concourse.masks import make_identity
+
+F32 = mybir.dt.float32
+BF16 = mybir.dt.bfloat16
+I32 = mybir.dt.int32
+U32 = mybir.dt.uint32
+U8 = mybir.dt.uint8
+FP8X4 = mybir.dt.float8_e4m3fn_x4
+ACT = mybir.ActivationFunctionType
+ALU = mybir.AluOpType
+
+P = 128
+PACK = 4
+K_PASS = P * PACK
+
+BATCH = 256
+PROTOS = 256
+INPUTS = 8192
+FEATURES = 1024
+
+COLS = BATCH + PROTOS
+GROUPS = INPUTS // K_PASS
+F_TILES = FEATURES // P
+HALF_TILES = PACK
+HALVES = F_TILES // HALF_TILES
+HALF_COLS = HALF_TILES * P
+ROW_TILES = BATCH // P
+
+RUN = 2
+BLOCKS = GROUPS // RUN
+PLANES = 4
+QUADS = GROUPS // PLANES
+PAIR = 2
+
+FLOPS = 2 * COLS * INPUTS * FEATURES + 3 * 2 * BATCH * PROTOS * FEATURES
+
+
+def tile_tverskylayer_pa_k_kernel(
+    tc,
+    x,
+    features_words,
+    features_scales,
+    prototypes_words,
+    prototypes_scales,
+    alpha,
+    beta,
+    theta,
+    out,
+):
+    nc = tc.nc
+    with ExitStack() as ctx:
+        ctx.enter_context(tc.manual_schedule())
+        keep = ctx.enter_context(tc.tile_pool(name="keep", bufs=1))
+        stage = ctx.enter_context(tc.tile_pool(name="stage", bufs=4))
+        psum = ctx.enter_context(tc.psum_pool(name="psum", bufs=4))
+
+        x_rows = x.rearrange("(r p) k -> p r k", p=P)
+        f_words = features_words.rearrange("g p n t -> p g (n t)").bitcast(I32)
+        p_words = prototypes_words.rearrange("g p n t -> p g (n t)").bitcast(I32)
+        f_scales = features_scales.bitcast(I32)
+        p_scales = prototypes_scales.bitcast(I32)
+
+        x_blk = [keep.tile([P, ROW_TILES, RUN * K_PASS], BF16, name="x%d" % b) for b in range(BLOCKS)]
+        mov_blk = [
+            keep.tile([P, RUN, COLS], U32, name="mov%d" % b, align_bytes=64) for b in range(BLOCKS)
+        ]
+        mov_planes = keep.tile([P, GROUPS, COLS], U8, name="mov_planes", align_bytes=64)
+        feat_first = [
+            keep.tile([P, RUN, HALF_COLS], U32, name="ff%d" % b, align_bytes=64)
+            for b in range(BLOCKS)
+        ]
+        feat_second = [
+            [
+                keep.tile([P, PLANES, PAIR * P], U32, name="fs%d_%d" % (pair, j), align_bytes=64)
+                for j in range(QUADS)
+            ]
+            for pair in range(HALF_TILES // PAIR)
+        ]
+        feat_planes = keep.tile([P, QUADS, FEATURES], U8, name="feat_planes", align_bytes=64)
+
+        ident = keep.tile([P, P], F32, name="ident")
+        make_identity(nc, ident[:])
+
+        nc.vector.memset(feat_planes[:].bitcast(I32), 0)
+        nc.vector.memset(mov_planes[:, :, BATCH:COLS].bitcast(I32), 0)
+
+        def load_feature_scales(j):
+            for quadrant in range(4):
+                nc.sync.dma_start(
+                    out=feat_planes[32 * quadrant : 32 * quadrant + 16, j, :].bitcast(I32),
+                    in_=f_scales[PLANES * j : PLANES * (j + 1), 4 * quadrant : 4 * quadrant + 4, :],
+                )
+
+        def load_prototype_scales():
+            for r in range(4):
+                nc.sync.dma_start(
+                    out=mov_planes[r:P:32, :, BATCH:COLS].bitcast(I32),
+                    in_=p_scales[:, r:16:4, :].rearrange("g q n -> q g n"),
+                )
+
+        for b in range(BLOCKS):
+            groups = slice(RUN * b, RUN * (b + 1))
+            nc.sync.dma_start(out=x_blk[b][:], in_=x_rows[:, :, K_PASS * RUN * b : K_PASS * RUN * (b + 1)])
+            if b == 0:
+                load_feature_scales(0)
+            elif b % 2 == 1 and (b + 1) // 2 < QUADS:
+                load_feature_scales((b + 1) // 2)
+            nc.sync.dma_start(out=mov_blk[b][:, :, BATCH:COLS].bitcast(I32), in_=p_words[:, groups, :])
+            nc.sync.dma_start(out=feat_first[b][:].bitcast(I32), in_=f_words[:, groups, 0:HALF_COLS])
+            if b == 0:
+                load_prototype_scales()
+        for pair in range(HALF_TILES // PAIR):
+            first_col = HALF_COLS + PAIR * P * pair
+            for j in range(QUADS):
+                nc.sync.dma_start(
+                    out=feat_second[pair][j][:].bitcast(I32),
+                    in_=f_words[:, PLANES * j : PLANES * (j + 1), first_col : first_col + PAIR * P],
+                )
+        theta_bf = keep.tile([P, 1], BF16, name="theta_bf")
+        alpha_bf = keep.tile([P, 1], BF16, name="alpha_bf")
+        beta_bf = keep.tile([P, 1], BF16, name="beta_bf")
+        nc.sync.dma_start(out=theta_bf[:], in_=theta.partition_broadcast(P))
+        nc.sync.dma_start(out=alpha_bf[:], in_=alpha.partition_broadcast(P))
+        nc.sync.dma_start(out=beta_bf[:], in_=beta.partition_broadcast(P))
+
+        def transpose_block(b):
+            words = x_blk[b][:].bitcast(F32)
+            banks = []
+            for i in range(RUN):
+                xt = psum.tile([P, 2, BATCH], F32, name="xt", tag="back")
+                for r in range(ROW_TILES):
+                    for u in range(2):
+                        nc.tensor.transpose(
+                            xt[:, u, P * r : P * (r + 1)],
+                            words[:, r, 256 * i + u : 256 * (i + 1) : 2],
+                            ident[:],
+                        )
+                banks.append(xt)
+            return banks
+
+        def quantise_block(b, banks):
+            for i in range(RUN):
+                g = RUN * b + i
+                grouped = stage.tile([P, BATCH, PACK], BF16, name="grouped", align_bytes=64)
+                pairs = grouped[:].rearrange("p c t -> p (c t)").bitcast(F32)
+                nc.scalar.copy(
+                    out=pairs.rearrange("p (c u) -> p c u", u=2),
+                    in_=banks[i][:].rearrange("p u c -> p c u"),
+                )
+                nc.vector.quantize_mx(
+                    out=mov_blk[b][:, i, 0:BATCH].bitcast(FP8X4),
+                    scales=mov_planes[:, g, 0:BATCH],
+                    in_=grouped[:].rearrange("p c t -> p (c t)"),
+                )
+
+        def first_stage_pass(acc, g, m, words):
+            first_row = PACK * (g % PLANES)
+            nc.tensor.matmul_mx(
+                out=acc[:],
+                lhsT=words.bitcast(FP8X4),
+                lhsT_scale=feat_planes[first_row:P, g // PLANES, P * m : P * (m + 1)],
+                rhs=mov_blk[g // RUN][:, g % RUN, :].bitcast(FP8X4),
+                rhs_scale=mov_planes[:, g, :],
+                start=(g == 0),
+                stop=(g == GROUPS - 1),
+            )
+
+        SLOT = BATCH
+        s2_values = [
+            keep.tile([P, 4 * SLOT, PACK], BF16, name="s2_values%d" % h, align_bytes=64)
+            for h in range(HALVES)
+        ]
+        s2_words = [
+            keep.tile([P, 4 * SLOT], U32, name="s2_words%d" % h, align_bytes=64) for h in range(HALVES)
+        ]
+        s2_planes = [
+            keep.tile([P, 4 * SLOT], U8, name="s2_planes%d" % h, align_bytes=64) for h in range(HALVES)
+        ]
+
+        def activations(acc, m):
+            h, t = m // HALF_TILES, m % HALF_TILES
+            pres = stage.tile([P, COLS], F32, name="pres")
+            nc.scalar.activation(out=pres[:], in_=acc[:], func=ACT.Relu)
+            nc.scalar.activation(out=s2_values[h][:, SLOT : 3 * SLOT, t], in_=pres[:], func=ACT.Square)
+            nc.vector.tensor_scalar(
+                out=s2_values[h][:].rearrange("p (s c) t -> p s c t", s=4)[:, 0:4:3, :, t],
+                in0=pres[:].rearrange("p (s c) -> p s c", s=2),
+                scalar1=-1.0,
+                scalar2=1.0,
+                op0=ALU.mult,
+                op1=ALU.add,
+            )
+
+        def quantise_half(h):
+            nc.vector.quantize_mx(
+                out=s2_words[h][:].bitcast(FP8X4),
+                scales=s2_planes[h][:],
+                in_=s2_values[h][:].rearrange("p c t -> p (c t)"),
+            )
+
+        def second_stage_pass(result, h, stationary_col, moving_cols):
+            stationary_cols = slice(stationary_col, stationary_col + P)
+            nc.tensor.matmul_mx(
+                out=result,
+                lhsT=s2_words[h][:, stationary_cols].bitcast(FP8X4),
+                lhsT_scale=s2_planes[h][:, stationary_cols],
+                rhs=s2_words[h][:, moving_cols].bitcast(FP8X4),
+                rhs_scale=s2_planes[h][:, moving_cols],
+                start=(h == 0),
+                stop=(h == HALVES - 1),
+            )
+
+        def second_stage(h, common_xd, pd):
+            for r in range(ROW_TILES):
+                second_stage_pass(common_xd[r][:], h, SLOT + P * r, slice(2 * SLOT, 4 * SLOT))
+                second_stage_pass(pd[r][:], h, P * r, slice(2 * SLOT, 3 * SLOT))
+
+        acc_first = [psum.tile([P, COLS], F32, name="acc%d" % m, tag="front") for m in range(HALF_TILES)]
+        banks = transpose_block(0)
+        for b in range(BLOCKS):
+            quantise_block(b, banks)
+            if b + 1 < BLOCKS:
+                banks = transpose_block(b + 1)
+            for i in range(RUN):
+                for m in range(HALF_TILES):
+                    first_stage_pass(acc_first[m], RUN * b + i, m, feat_first[b][:, i, P * m : P * (m + 1)])
+
+        for m in range(HALF_TILES):
+            activations(acc_first[m], m)
+        quantise_half(0)
+
+        weights = keep.tile([P, 3], F32, name="weights")
+        nc.vector.tensor_copy(out=weights[:, 0:1], in_=theta_bf[:])
+        nc.vector.tensor_scalar(out=weights[:, 1:2], in0=alpha_bf[:], scalar1=-1.0, scalar2=None, op0=ALU.mult)
+        nc.vector.tensor_scalar(out=weights[:, 2:3], in0=beta_bf[:], scalar1=-1.0, scalar2=None, op0=ALU.mult)
+
+        common_xd = []
+        pd = []
+        for m in range(HALF_TILES, F_TILES):
+            acc = psum.tile([P, COLS], F32, name="acc_second", tag="back")
+            pair, in_pair = (m - HALF_TILES) // PAIR, (m - HALF_TILES) % PAIR
+            for g in range(GROUPS):
+                words = feat_second[pair][g // PLANES][:, g % PLANES, P * in_pair : P * (in_pair + 1)]
+                first_stage_pass(acc, g, m, words)
+            activations(acc, m)
+            if m == F_TILES - 2:
+                common_xd = [
+                    psum.tile([P, 2 * SLOT], F32, name="common_xd%d" % r, tag="front")
+                    for r in range(ROW_TILES)
+                ]
+                pd = [psum.tile([P, SLOT], F32, name="pd%d" % r, tag="front") for r in range(ROW_TILES)]
+                second_stage(0, common_xd, pd)
+        quantise_half(1)
+        second_stage(1, common_xd, pd)
+
+        for r in range(ROW_TILES):
+            part = stage.tile([P, PROTOS], F32, name="part")
+            nc.scalar.activation(out=part[:], in_=common_xd[r][:, 0:SLOT], func=ACT.Copy, scale=weights[:, 0:1])
+            both = stage.tile([P, PROTOS], F32, name="both")
+            nc.vector.scalar_tensor_tensor(
+                out=both[:],
+                in0=common_xd[r][:, SLOT : 2 * SLOT],
+                scalar=weights[:, 1:2],
+                in1=part[:],
+                op0=ALU.mult,
+                op1=ALU.add,
+            )
+            result = stage.tile([P, PROTOS], F32, name="result")
+            nc.vector.scalar_tensor_tensor(
+                out=result[:],
+                in0=pd[r][:],
+                scalar=weights[:, 2:3],
+                in1=both[:],
+                op0=ALU.mult,
+                op1=ALU.add,
+            )
+            nc.sync.dma_start(out=out[P * r : P * (r + 1), :], in_=result[:])

@@ -101,9 +101,14 @@ def tile_tverskylayer_pa_k_kernel(
                     in_=p_scales[:, r:16:4, :].rearrange("g q n -> q g n"),
                 )
 
+        def load_x(b):
+            nc.sync.dma_start(out=x_blk[b][:], in_=x_rows[:, :, K_PASS * RUN * b : K_PASS * RUN * (b + 1)])
+
+        load_x(0)
         for b in range(BLOCKS):
             groups = slice(RUN * b, RUN * (b + 1))
-            nc.sync.dma_start(out=x_blk[b][:], in_=x_rows[:, :, K_PASS * RUN * b : K_PASS * RUN * (b + 1)])
+            if b + 1 < BLOCKS:
+                load_x(b + 1)
             if b == 0:
                 load_feature_scales(0)
             elif b % 2 == 1 and (b + 1) // 2 < QUADS:
@@ -127,16 +132,17 @@ def tile_tverskylayer_pa_k_kernel(
         nc.sync.dma_start(out=beta_bf[:], in_=beta.partition_broadcast(P))
 
         def transpose_block(b):
-            words = x_blk[b][:].bitcast(F32)
+            words = x_blk[b][:].bitcast(F32).rearrange("p r (i w u) -> p r i u w", i=RUN, u=2)
+            sorted_words = stage.tile([P, ROW_TILES, RUN, 2, P], F32, name="sorted_words")
+            nc.vector.tensor_copy(out=sorted_words[:, 0], in_=words[:, 0])
+            nc.scalar.copy(out=sorted_words[:, 1], in_=words[:, 1])
             banks = []
             for i in range(RUN):
                 xt = psum.tile([P, 2, BATCH], F32, name="xt", tag="back")
                 for r in range(ROW_TILES):
                     for u in range(2):
                         nc.tensor.transpose(
-                            xt[:, u, P * r : P * (r + 1)],
-                            words[:, r, 256 * i + u : 256 * (i + 1) : 2],
-                            ident[:],
+                            xt[:, u, P * r : P * (r + 1)], sorted_words[:, r, i, u, :], ident[:]
                         )
                 banks.append(xt)
             return banks

@@ -34,6 +34,9 @@ BLOCKS = GROUPS // RUN
 PLANES = 4
 QUADS = GROUPS // PLANES
 PAIR = 2
+X_SIDE = 0
+P_SIDE = 1
+SIDE_COLS = COLS // 2
 
 FLOPS = 2 * COLS * INPUTS * FEATURES + 3 * 2 * BATCH * PROTOS * FEATURES
 
@@ -127,15 +130,18 @@ def tile_tverskylayer_pa_k_kernel(
         theta_bf = keep.tile([P, 1], BF16, name="theta_bf")
         alpha_bf = keep.tile([P, 1], BF16, name="alpha_bf")
         beta_bf = keep.tile([P, 1], BF16, name="beta_bf")
-        nc.sync.dma_start(out=theta_bf[:], in_=theta.partition_broadcast(P))
-        nc.sync.dma_start(out=alpha_bf[:], in_=alpha.partition_broadcast(P))
-        nc.sync.dma_start(out=beta_bf[:], in_=beta.partition_broadcast(P))
+        nc.gpsimd.dma_start(out=theta_bf[:], in_=theta.partition_broadcast(P))
+        nc.gpsimd.dma_start(out=alpha_bf[:], in_=alpha.partition_broadcast(P))
+        nc.gpsimd.dma_start(out=beta_bf[:], in_=beta.partition_broadcast(P))
 
-        def transpose_block(b):
+        def sort_block(b):
             words = x_blk[b][:].bitcast(F32).rearrange("p r (i w u) -> p r i u w", i=RUN, u=2)
             sorted_words = stage.tile([P, ROW_TILES, RUN, 2, P], F32, name="sorted_words")
             nc.vector.tensor_copy(out=sorted_words[:, 0], in_=words[:, 0])
             nc.scalar.copy(out=sorted_words[:, 1], in_=words[:, 1])
+            return sorted_words
+
+        def transpose_block(sorted_words):
             banks = []
             for i in range(RUN):
                 xt = psum.tile([P, 2, BATCH], F32, name="xt", tag="back")
@@ -162,19 +168,19 @@ def tile_tverskylayer_pa_k_kernel(
                     in_=grouped[:].rearrange("p c t -> p (c t)"),
                 )
 
-        def first_stage_pass(acc, g, m, words):
+        def first_stage_pass(acc, g, m, words, cols):
             first_row = PACK * (g % PLANES)
             nc.tensor.matmul_mx(
-                out=acc[:],
+                out=acc,
                 lhsT=words.bitcast(FP8X4),
                 lhsT_scale=feat_planes[first_row:P, g // PLANES, P * m : P * (m + 1)],
-                rhs=mov_blk[g // RUN][:, g % RUN, :].bitcast(FP8X4),
-                rhs_scale=mov_planes[:, g, :],
+                rhs=mov_blk[g // RUN][:, g % RUN, cols].bitcast(FP8X4),
+                rhs_scale=mov_planes[:, g, cols],
                 start=(g == 0),
                 stop=(g == GROUPS - 1),
             )
 
-        SLOT = BATCH
+        SLOT = SIDE_COLS
         s2_values = [
             keep.tile([P, 4 * SLOT, PACK], BF16, name="s2_values%d" % h, align_bytes=64)
             for h in range(HALVES)
@@ -186,25 +192,32 @@ def tile_tverskylayer_pa_k_kernel(
             keep.tile([P, 4 * SLOT], U8, name="s2_planes%d" % h, align_bytes=64) for h in range(HALVES)
         ]
 
-        def activations(acc, m):
+        def activations(sums, m, side):
             h, t = m // HALF_TILES, m % HALF_TILES
-            pres = stage.tile([P, COLS], F32, name="pres")
-            nc.scalar.activation(out=pres[:], in_=acc[:], func=ACT.Relu)
-            nc.scalar.activation(out=s2_values[h][:, SLOT : 3 * SLOT, t], in_=pres[:], func=ACT.Square)
+            square_slot = 1 + side
+            rest_slot = 3 * side
+            pres = stage.tile([P, SLOT], F32, name="pres")
+            nc.scalar.activation(out=pres[:], in_=sums, func=ACT.Relu)
+            squares = s2_values[h][:, SLOT * square_slot : SLOT * (square_slot + 1), t]
+            if side == X_SIDE:
+                nc.scalar.activation(out=squares, in_=pres[:], func=ACT.Square)
+            else:
+                nc.vector.tensor_tensor(out=squares, in0=pres[:], in1=pres[:], op=ALU.mult)
             nc.vector.tensor_scalar(
-                out=s2_values[h][:].rearrange("p (s c) t -> p s c t", s=4)[:, 0:4:3, :, t],
-                in0=pres[:].rearrange("p (s c) -> p s c", s=2),
+                out=s2_values[h][:, SLOT * rest_slot : SLOT * (rest_slot + 1), t],
+                in0=pres[:],
                 scalar1=-1.0,
                 scalar2=1.0,
                 op0=ALU.mult,
                 op1=ALU.add,
             )
 
-        def quantise_half(h):
+        def quantise_side(h, side):
+            cols = slice(2 * SLOT * side, 2 * SLOT * (side + 1))
             nc.vector.quantize_mx(
-                out=s2_words[h][:].bitcast(FP8X4),
-                scales=s2_planes[h][:],
-                in_=s2_values[h][:].rearrange("p c t -> p (c t)"),
+                out=s2_words[h][:, cols].bitcast(FP8X4),
+                scales=s2_planes[h][:, cols],
+                in_=s2_values[h][:, cols, :].rearrange("p c t -> p (c t)"),
             )
 
         def second_stage_pass(result, h, stationary_col, moving_cols):
@@ -225,18 +238,22 @@ def tile_tverskylayer_pa_k_kernel(
                 second_stage_pass(pd[r][:], h, P * r, slice(2 * SLOT, 3 * SLOT))
 
         acc_first = [psum.tile([P, COLS], F32, name="acc%d" % m, tag="front") for m in range(HALF_TILES)]
-        banks = transpose_block(0)
+        banks = transpose_block(sort_block(0))
         for b in range(BLOCKS):
+            if b + 1 < BLOCKS:
+                sorted_words = sort_block(b + 1)
             quantise_block(b, banks)
             if b + 1 < BLOCKS:
-                banks = transpose_block(b + 1)
+                banks = transpose_block(sorted_words)
             for i in range(RUN):
                 for m in range(HALF_TILES):
-                    first_stage_pass(acc_first[m], RUN * b + i, m, feat_first[b][:, i, P * m : P * (m + 1)])
+                    words = feat_first[b][:, i, P * m : P * (m + 1)]
+                    first_stage_pass(acc_first[m][:], RUN * b + i, m, words, slice(0, COLS))
 
-        for m in range(HALF_TILES):
-            activations(acc_first[m], m)
-        quantise_half(0)
+        for side in (P_SIDE, X_SIDE):
+            for m in range(HALF_TILES):
+                activations(acc_first[m][:, SIDE_COLS * side : SIDE_COLS * (side + 1)], m, side)
+            quantise_side(0, side)
 
         weights = keep.tile([P, 3], F32, name="weights")
         nc.vector.tensor_copy(out=weights[:, 0:1], in_=theta_bf[:])
@@ -245,21 +262,22 @@ def tile_tverskylayer_pa_k_kernel(
 
         common_xd = []
         pd = []
-        for m in range(HALF_TILES, F_TILES):
-            acc = psum.tile([P, COLS], F32, name="acc_second", tag="back")
-            pair, in_pair = (m - HALF_TILES) // PAIR, (m - HALF_TILES) % PAIR
-            for g in range(GROUPS):
-                words = feat_second[pair][g // PLANES][:, g % PLANES, P * in_pair : P * (in_pair + 1)]
-                first_stage_pass(acc, g, m, words)
-            activations(acc, m)
-            if m == F_TILES - 2:
-                common_xd = [
-                    psum.tile([P, 2 * SLOT], F32, name="common_xd%d" % r, tag="front")
-                    for r in range(ROW_TILES)
-                ]
-                pd = [psum.tile([P, SLOT], F32, name="pd%d" % r, tag="front") for r in range(ROW_TILES)]
-                second_stage(0, common_xd, pd)
-        quantise_half(1)
+        for side in (P_SIDE, X_SIDE):
+            for m in range(HALF_TILES, F_TILES):
+                acc = psum.tile([P, SIDE_COLS], F32, name="acc_second", tag="back")
+                pair, in_pair = (m - HALF_TILES) // PAIR, (m - HALF_TILES) % PAIR
+                for g in range(GROUPS):
+                    words = feat_second[pair][g // PLANES][:, g % PLANES, P * in_pair : P * (in_pair + 1)]
+                    first_stage_pass(acc[:], g, m, words, slice(SIDE_COLS * side, SIDE_COLS * (side + 1)))
+                activations(acc[:], m, side)
+                if side == X_SIDE and m == F_TILES - 2:
+                    common_xd = [
+                        psum.tile([P, 2 * SLOT], F32, name="common_xd%d" % r, tag="front")
+                        for r in range(ROW_TILES)
+                    ]
+                    pd = [psum.tile([P, SLOT], F32, name="pd%d" % r, tag="front") for r in range(ROW_TILES)]
+                    second_stage(0, common_xd, pd)
+            quantise_side(1, side)
         second_stage(1, common_xd, pd)
 
         for r in range(ROW_TILES):

@@ -130,9 +130,9 @@ def tile_tverskylayer_pa_k_kernel(
         theta_bf = keep.tile([P, 1], BF16, name="theta_bf")
         alpha_bf = keep.tile([P, 1], BF16, name="alpha_bf")
         beta_bf = keep.tile([P, 1], BF16, name="beta_bf")
-        nc.gpsimd.dma_start(out=theta_bf[:], in_=theta.partition_broadcast(P))
-        nc.gpsimd.dma_start(out=alpha_bf[:], in_=alpha.partition_broadcast(P))
-        nc.gpsimd.dma_start(out=beta_bf[:], in_=beta.partition_broadcast(P))
+        nc.sync.dma_start(out=theta_bf[:], in_=theta.partition_broadcast(P))
+        nc.sync.dma_start(out=alpha_bf[:], in_=alpha.partition_broadcast(P))
+        nc.sync.dma_start(out=beta_bf[:], in_=beta.partition_broadcast(P))
 
         def sort_block(b):
             words = x_blk[b][:].bitcast(F32).rearrange("p r (i w u) -> p r i u w", i=RUN, u=2)

@@ -29,11 +29,15 @@ HALVES = F_TILES // HALF_TILES
 HALF_COLS = HALF_TILES * P
 ROW_TILES = BATCH // P
 
-RUN = 2
-BLOCKS = GROUPS // RUN
+EARLY_TILES = 6
+LATE_TILES = F_TILES - EARLY_TILES
+EARLY_COLS = EARLY_TILES * P
+BLOCK_SIZES = [1, 1] + 7 * [2]
+BLOCK_STARTS = [sum(BLOCK_SIZES[:b]) for b in range(len(BLOCK_SIZES))]
+BLOCKS = len(BLOCK_SIZES)
 PLANES = 4
 QUADS = GROUPS // PLANES
-PAIR = 2
+PASSES_BEFORE_TRANSPOSES = 3
 X_SIDE = 0
 P_SIDE = 1
 SIDE_COLS = COLS // 2
@@ -58,7 +62,8 @@ def tile_tverskylayer_pa_k_kernel(
         ctx.enter_context(tc.manual_schedule())
         keep = ctx.enter_context(tc.tile_pool(name="keep", bufs=1))
         stage = ctx.enter_context(tc.tile_pool(name="stage", bufs=4))
-        psum = ctx.enter_context(tc.psum_pool(name="psum", bufs=4))
+        psum_early = ctx.enter_context(tc.psum_pool(name="psum_early", bufs=EARLY_TILES))
+        psum_late = ctx.enter_context(tc.psum_pool(name="psum_late", bufs=LATE_TILES))
 
         x_rows = x.rearrange("(r p) k -> p r k", p=P)
         f_words = features_words.rearrange("g p n t -> p g (n t)").bitcast(I32)
@@ -66,29 +71,25 @@ def tile_tverskylayer_pa_k_kernel(
         f_scales = features_scales.bitcast(I32)
         p_scales = prototypes_scales.bitcast(I32)
 
-        x_blk = [keep.tile([P, ROW_TILES, RUN * K_PASS], BF16, name="x%d" % b) for b in range(BLOCKS)]
+        x_blk = [
+            keep.tile([P, ROW_TILES, size * K_PASS], BF16, name="x%d" % b) for b, size in enumerate(BLOCK_SIZES)
+        ]
         mov_blk = [
-            keep.tile([P, RUN, COLS], U32, name="mov%d" % b, align_bytes=64) for b in range(BLOCKS)
+            keep.tile([P, size, COLS], U32, name="mov%d" % b, align_bytes=64) for b, size in enumerate(BLOCK_SIZES)
         ]
         mov_planes = keep.tile([P, GROUPS, COLS], U8, name="mov_planes", align_bytes=64)
-        feat_first = [
-            keep.tile([P, RUN, HALF_COLS], U32, name="ff%d" % b, align_bytes=64)
-            for b in range(BLOCKS)
-        ]
-        feat_second = [
-            [
-                keep.tile([P, PLANES, PAIR * P], U32, name="fs%d_%d" % (pair, j), align_bytes=64)
-                for j in range(QUADS)
-            ]
-            for pair in range(HALF_TILES // PAIR)
+        feat_early = [keep.tile([P, EARLY_COLS], U32, name="fe%d" % g, align_bytes=64) for g in range(GROUPS)]
+        feat_late = [
+            keep.tile([P, PLANES, LATE_TILES * P], U32, name="fl%d" % j, align_bytes=64) for j in range(QUADS)
         ]
         feat_planes = keep.tile([P, QUADS, FEATURES], U8, name="feat_planes", align_bytes=64)
 
         ident = keep.tile([P, P], F32, name="ident")
         make_identity(nc, ident[:])
 
-        nc.vector.memset(feat_planes[:].bitcast(I32), 0)
+        nc.vector.memset(feat_planes[:, 0, :].bitcast(I32), 0)
         nc.vector.memset(mov_planes[:, :, BATCH:COLS].bitcast(I32), 0)
+        nc.gpsimd.memset(feat_planes[:, 1:QUADS, :].bitcast(I32), 0)
 
         def load_feature_scales(j):
             for quadrant in range(4):
@@ -105,28 +106,32 @@ def tile_tverskylayer_pa_k_kernel(
                 )
 
         def load_x(b):
-            nc.sync.dma_start(out=x_blk[b][:], in_=x_rows[:, :, K_PASS * RUN * b : K_PASS * RUN * (b + 1)])
+            first_k = K_PASS * BLOCK_STARTS[b]
+            nc.sync.dma_start(out=x_blk[b][:], in_=x_rows[:, :, first_k : first_k + K_PASS * BLOCK_SIZES[b]])
 
         load_x(0)
         for b in range(BLOCKS):
-            groups = slice(RUN * b, RUN * (b + 1))
-            if b + 1 < BLOCKS:
-                load_x(b + 1)
+            first, size = BLOCK_STARTS[b], BLOCK_SIZES[b]
             if b == 0:
                 load_feature_scales(0)
-            elif b % 2 == 1 and (b + 1) // 2 < QUADS:
-                load_feature_scales((b + 1) // 2)
-            nc.sync.dma_start(out=mov_blk[b][:, :, BATCH:COLS].bitcast(I32), in_=p_words[:, groups, :])
-            nc.sync.dma_start(out=feat_first[b][:].bitcast(I32), in_=f_words[:, groups, 0:HALF_COLS])
-            if b == 0:
-                load_prototype_scales()
-        for pair in range(HALF_TILES // PAIR):
-            first_col = HALF_COLS + PAIR * P * pair
-            for j in range(QUADS):
-                nc.sync.dma_start(
-                    out=feat_second[pair][j][:].bitcast(I32),
-                    in_=f_words[:, PLANES * j : PLANES * (j + 1), first_col : first_col + PAIR * P],
-                )
+            nc.sync.dma_start(
+                out=mov_blk[b][:, :, BATCH:COLS].bitcast(I32), in_=p_words[:, first : first + size, :]
+            )
+            for g in range(first, first + size):
+                nc.sync.dma_start(out=feat_early[g][:].bitcast(I32), in_=f_words[:, g, 0:EARLY_COLS])
+                if g == first:
+                    if b == 0:
+                        load_prototype_scales()
+                    if b + 1 < BLOCKS:
+                        load_x(b + 1)
+            if b == 1:
+                for j in range(1, QUADS):
+                    load_feature_scales(j)
+        for j in range(QUADS):
+            nc.sync.dma_start(
+                out=feat_late[j][:].bitcast(I32),
+                in_=f_words[:, PLANES * j : PLANES * (j + 1), EARLY_COLS:FEATURES],
+            )
         theta_bf = keep.tile([P, 1], BF16, name="theta_bf")
         alpha_bf = keep.tile([P, 1], BF16, name="alpha_bf")
         beta_bf = keep.tile([P, 1], BF16, name="beta_bf")
@@ -135,27 +140,28 @@ def tile_tverskylayer_pa_k_kernel(
         nc.sync.dma_start(out=beta_bf[:], in_=beta.partition_broadcast(P))
 
         def sort_block(b):
-            words = x_blk[b][:].bitcast(F32).rearrange("p r (i w u) -> p r i u w", i=RUN, u=2)
-            sorted_words = stage.tile([P, ROW_TILES, RUN, 2, P], F32, name="sorted_words")
-            nc.vector.tensor_copy(out=sorted_words[:, 0], in_=words[:, 0])
-            nc.scalar.copy(out=sorted_words[:, 1], in_=words[:, 1])
+            size = BLOCK_SIZES[b]
+            sorted_words = stage.tile([P, ROW_TILES * size, 2, P], F32, name="sorted_words")
+            nc.vector.tensor_copy(
+                out=sorted_words[:],
+                in_=x_blk[b][:].rearrange("p r k -> p (r k)").bitcast(F32).rearrange("p (i w u) -> p i u w", w=P, u=2),
+            )
             return sorted_words
 
-        def transpose_block(sorted_words):
+        def transpose_block(b, sorted_words):
             banks = []
-            for i in range(RUN):
-                xt = psum.tile([P, 2, BATCH], F32, name="xt", tag="back")
+            for i in range(BLOCK_SIZES[b]):
+                xt = psum_late.tile([P, 2, BATCH], F32, name="xt", tag="late")
                 for r in range(ROW_TILES):
                     for u in range(2):
                         nc.tensor.transpose(
-                            xt[:, u, P * r : P * (r + 1)], sorted_words[:, r, i, u, :], ident[:]
+                            xt[:, u, P * r : P * (r + 1)], sorted_words[:, BLOCK_SIZES[b] * r + i, u, :], ident[:]
                         )
                 banks.append(xt)
             return banks
 
         def quantise_block(b, banks):
-            for i in range(RUN):
-                g = RUN * b + i
+            for i in range(BLOCK_SIZES[b]):
                 grouped = stage.tile([P, BATCH, PACK], BF16, name="grouped", align_bytes=64)
                 pairs = grouped[:].rearrange("p c t -> p (c t)").bitcast(F32)
                 nc.scalar.copy(
@@ -164,23 +170,33 @@ def tile_tverskylayer_pa_k_kernel(
                 )
                 nc.vector.quantize_mx(
                     out=mov_blk[b][:, i, 0:BATCH].bitcast(FP8X4),
-                    scales=mov_planes[:, g, 0:BATCH],
+                    scales=mov_planes[:, BLOCK_STARTS[b] + i, 0:BATCH],
                     in_=grouped[:].rearrange("p c t -> p (c t)"),
                 )
 
-        def first_stage_pass(acc, g, m, words, cols):
+        def block_of(g):
+            return max(b for b in range(BLOCKS) if BLOCK_STARTS[b] <= g)
+
+        def first_stage_pass(acc, g, m, cols):
+            b = block_of(g)
             first_row = PACK * (g % PLANES)
+            if m < EARLY_TILES:
+                words = feat_early[g][:, P * m : P * (m + 1)]
+            else:
+                words = feat_late[g // PLANES][:, g % PLANES, P * (m - EARLY_TILES) : P * (m - EARLY_TILES + 1)]
             nc.tensor.matmul_mx(
                 out=acc,
                 lhsT=words.bitcast(FP8X4),
                 lhsT_scale=feat_planes[first_row:P, g // PLANES, P * m : P * (m + 1)],
-                rhs=mov_blk[g // RUN][:, g % RUN, cols].bitcast(FP8X4),
+                rhs=mov_blk[b][:, g - BLOCK_STARTS[b], cols].bitcast(FP8X4),
                 rhs_scale=mov_planes[:, g, cols],
                 start=(g == 0),
                 stop=(g == GROUPS - 1),
             )
 
+        pres = [keep.tile([P, HALF_TILES, COLS], F32, name="pres%d" % h) for h in range(HALVES)]
         SLOT = SIDE_COLS
+        REST_X, SQUARE_X, SQUARE_P, REST_P = 0, SLOT, 2 * SLOT, 3 * SLOT
         s2_values = [
             keep.tile([P, 4 * SLOT, PACK], BF16, name="s2_values%d" % h, align_bytes=64)
             for h in range(HALVES)
@@ -192,38 +208,43 @@ def tile_tverskylayer_pa_k_kernel(
             keep.tile([P, 4 * SLOT], U8, name="s2_planes%d" % h, align_bytes=64) for h in range(HALVES)
         ]
 
-        def activations(sums, m, side):
-            h, t = m // HALF_TILES, m % HALF_TILES
-            square_slot = 1 + side
-            rest_slot = 3 * side
-            pres = stage.tile([P, SLOT], F32, name="pres")
-            nc.scalar.activation(out=pres[:], in_=sums, func=ACT.Relu)
-            squares = s2_values[h][:, SLOT * square_slot : SLOT * (square_slot + 1), t]
-            if side == X_SIDE:
-                nc.scalar.activation(out=squares, in_=pres[:], func=ACT.Square)
+        def relu(sums, m, cols):
+            nc.scalar.activation(out=pres[m // HALF_TILES][:, m % HALF_TILES, cols], in_=sums, func=ACT.Relu)
+
+        def presences(h, first_col, width):
+            return pres[h][:, :, first_col : first_col + width].rearrange("p t c -> p c t")
+
+        def square(h, slot, first_col, width, engine):
+            values = s2_values[h][:, slot + first_col % SLOT : slot + first_col % SLOT + width, :]
+            source = presences(h, first_col, width)
+            if engine is nc.scalar:
+                nc.scalar.activation(out=values, in_=source, func=ACT.Square)
             else:
-                nc.vector.tensor_tensor(out=squares, in0=pres[:], in1=pres[:], op=ALU.mult)
+                nc.vector.tensor_tensor(out=values, in0=source, in1=source, op=ALU.mult)
+
+        def rest(h, slot, first_col, width):
             nc.vector.tensor_scalar(
-                out=s2_values[h][:, SLOT * rest_slot : SLOT * (rest_slot + 1), t],
-                in0=pres[:],
+                out=s2_values[h][:, slot + first_col % SLOT : slot + first_col % SLOT + width, :],
+                in0=presences(h, first_col, width),
                 scalar1=-1.0,
                 scalar2=1.0,
                 op0=ALU.mult,
                 op1=ALU.add,
             )
 
-        def quantise_side(h, side):
-            cols = slice(2 * SLOT * side, 2 * SLOT * (side + 1))
+        def quantise(h, first_col, width):
+            cols = slice(first_col, first_col + width)
             nc.vector.quantize_mx(
                 out=s2_words[h][:, cols].bitcast(FP8X4),
                 scales=s2_planes[h][:, cols],
                 in_=s2_values[h][:, cols, :].rearrange("p c t -> p (c t)"),
             )
 
-        def second_stage_pass(result, h, stationary_col, moving_cols):
+        def second_stage_pass(result, h, stationary_col, moving_col):
             stationary_cols = slice(stationary_col, stationary_col + P)
+            moving_cols = slice(moving_col, moving_col + SLOT)
             nc.tensor.matmul_mx(
-                out=result,
+                out=result[:],
                 lhsT=s2_words[h][:, stationary_cols].bitcast(FP8X4),
                 lhsT_scale=s2_planes[h][:, stationary_cols],
                 rhs=s2_words[h][:, moving_cols].bitcast(FP8X4),
@@ -232,73 +253,77 @@ def tile_tverskylayer_pa_k_kernel(
                 stop=(h == HALVES - 1),
             )
 
-        def second_stage(h, common_xd, pd):
-            for r in range(ROW_TILES):
-                second_stage_pass(common_xd[r][:], h, SLOT + P * r, slice(2 * SLOT, 4 * SLOT))
-                second_stage_pass(pd[r][:], h, P * r, slice(2 * SLOT, 3 * SLOT))
+        def second_stage(h, r):
+            second_stage_pass(pd[r], h, REST_X + P * r, SQUARE_P)
+            second_stage_pass(xd[r], h, SQUARE_X + P * r, REST_P)
+            second_stage_pass(common[r], h, SQUARE_X + P * r, SQUARE_P)
 
-        acc_first = [psum.tile([P, COLS], F32, name="acc%d" % m, tag="front") for m in range(HALF_TILES)]
-        banks = transpose_block(sort_block(0))
-        for b in range(BLOCKS):
-            if b + 1 < BLOCKS:
-                sorted_words = sort_block(b + 1)
-            quantise_block(b, banks)
-            if b + 1 < BLOCKS:
-                banks = transpose_block(sorted_words)
-            for i in range(RUN):
-                for m in range(HALF_TILES):
-                    words = feat_first[b][:, i, P * m : P * (m + 1)]
-                    first_stage_pass(acc_first[m][:], RUN * b + i, m, words, slice(0, COLS))
+        accs = [psum_early.tile([P, COLS], F32, name="acc%d" % m, tag="early") for m in range(EARLY_TILES)]
+        banks = transpose_block(0, sort_block(0))
+        quantise_block(0, banks)
+        sorted_words = sort_block(1)
+        for b in range(BLOCKS - 1):
+            passes = [(g, m) for g in range(BLOCK_STARTS[b], BLOCK_STARTS[b + 1]) for m in range(EARLY_TILES)]
+            for g, m in passes[:PASSES_BEFORE_TRANSPOSES]:
+                first_stage_pass(accs[m][:], g, m, slice(0, COLS))
+            banks = transpose_block(b + 1, sorted_words)
+            quantise_block(b + 1, banks)
+            if b + 2 < BLOCKS:
+                sorted_words = sort_block(b + 2)
+            for g, m in passes[PASSES_BEFORE_TRANSPOSES:]:
+                first_stage_pass(accs[m][:], g, m, slice(0, COLS))
+        for m in range(EARLY_TILES):
+            for g in range(BLOCK_STARTS[BLOCKS - 1], GROUPS):
+                first_stage_pass(accs[m][:], g, m, slice(0, COLS))
+            relu(accs[m][:], m, slice(0, COLS))
 
-        for side in (P_SIDE, X_SIDE):
-            for m in range(HALF_TILES):
-                activations(acc_first[m][:, SIDE_COLS * side : SIDE_COLS * (side + 1)], m, side)
-            quantise_side(0, side)
+        square(0, SQUARE_X, 0, SLOT, nc.scalar)
+        square(0, SQUARE_P, SLOT, SLOT, nc.vector)
+        rest(0, REST_P, SLOT, SLOT)
+        rest(0, REST_X, 0, SLOT)
+        quantise(0, SQUARE_P, 2 * SLOT)
+        quantise(0, REST_X, 2 * SLOT)
 
         weights = keep.tile([P, 3], F32, name="weights")
         nc.vector.tensor_copy(out=weights[:, 0:1], in_=theta_bf[:])
         nc.vector.tensor_scalar(out=weights[:, 1:2], in0=alpha_bf[:], scalar1=-1.0, scalar2=None, op0=ALU.mult)
         nc.vector.tensor_scalar(out=weights[:, 2:3], in0=beta_bf[:], scalar1=-1.0, scalar2=None, op0=ALU.mult)
 
-        common_xd = []
-        pd = []
-        for side in (P_SIDE, X_SIDE):
-            for m in range(HALF_TILES, F_TILES):
-                acc = psum.tile([P, SIDE_COLS], F32, name="acc_second", tag="back")
-                pair, in_pair = (m - HALF_TILES) // PAIR, (m - HALF_TILES) % PAIR
-                for g in range(GROUPS):
-                    words = feat_second[pair][g // PLANES][:, g % PLANES, P * in_pair : P * (in_pair + 1)]
-                    first_stage_pass(acc[:], g, m, words, slice(SIDE_COLS * side, SIDE_COLS * (side + 1)))
-                activations(acc[:], m, side)
-                if side == X_SIDE and m == F_TILES - 2:
-                    common_xd = [
-                        psum.tile([P, 2 * SLOT], F32, name="common_xd%d" % r, tag="front")
-                        for r in range(ROW_TILES)
-                    ]
-                    pd = [psum.tile([P, SLOT], F32, name="pd%d" % r, tag="front") for r in range(ROW_TILES)]
-                    second_stage(0, common_xd, pd)
-            quantise_side(1, side)
-        second_stage(1, common_xd, pd)
+        def late_passes(m, first_col, width):
+            acc = psum_late.tile([P, width], F32, name="acc_late", tag="late")
+            for g in range(GROUPS):
+                first_stage_pass(acc[:], g, m, slice(first_col, first_col + width))
+            relu(acc[:], m, slice(first_col, first_col + width))
 
+        for m in range(EARLY_TILES, F_TILES):
+            late_passes(m, SLOT, SLOT)
+        square(1, SQUARE_P, SLOT, SLOT, nc.scalar)
+        rest(1, REST_P, SLOT, SLOT)
+        quantise(1, SQUARE_P, 2 * SLOT)
+        for m in range(EARLY_TILES, F_TILES - 1):
+            late_passes(m, 0, SLOT)
         for r in range(ROW_TILES):
+            late_passes(F_TILES - 1, P * r, P)
+            square(1, SQUARE_X, P * r, P, nc.scalar)
+            rest(1, REST_X, P * r, P)
+            quantise(1, REST_X + P * r, P)
+            quantise(1, SQUARE_X + P * r, P)
+
+        pd = [psum_early.tile([P, SLOT], F32, name="pd%d" % r, tag="early") for r in range(ROW_TILES)]
+        xd = [psum_early.tile([P, SLOT], F32, name="xd%d" % r, tag="early") for r in range(ROW_TILES)]
+        common = [psum_early.tile([P, SLOT], F32, name="common%d" % r, tag="early") for r in range(ROW_TILES)]
+        for r in range(ROW_TILES):
+            second_stage(0, r)
+        for r in range(ROW_TILES):
+            second_stage(1, r)
             part = stage.tile([P, PROTOS], F32, name="part")
-            nc.scalar.activation(out=part[:], in_=common_xd[r][:, 0:SLOT], func=ACT.Copy, scale=weights[:, 0:1])
+            nc.scalar.activation(out=part[:], in_=pd[r][:], func=ACT.Copy, scale=weights[:, 2:3])
             both = stage.tile([P, PROTOS], F32, name="both")
             nc.vector.scalar_tensor_tensor(
-                out=both[:],
-                in0=common_xd[r][:, SLOT : 2 * SLOT],
-                scalar=weights[:, 1:2],
-                in1=part[:],
-                op0=ALU.mult,
-                op1=ALU.add,
+                out=both[:], in0=xd[r][:], scalar=weights[:, 1:2], in1=part[:], op0=ALU.mult, op1=ALU.add
             )
             result = stage.tile([P, PROTOS], F32, name="result")
             nc.vector.scalar_tensor_tensor(
-                out=result[:],
-                in0=pd[r][:],
-                scalar=weights[:, 2:3],
-                in1=both[:],
-                op0=ALU.mult,
-                op1=ALU.add,
+                out=result[:], in0=common[r][:], scalar=weights[:, 0:1], in1=both[:], op0=ALU.mult, op1=ALU.add
             )
             nc.sync.dma_start(out=out[P * r : P * (r + 1), :], in_=result[:])

@@ -37,7 +37,7 @@ BLOCK_STARTS = [sum(BLOCK_SIZES[:b]) for b in range(len(BLOCK_SIZES))]
 BLOCKS = len(BLOCK_SIZES)
 PLANES = 4
 QUADS = GROUPS // PLANES
-PASSES_BEFORE_TRANSPOSES = 3
+PASSES_BEFORE_TRANSPOSES = [0] + 8 * [3]
 X_SIDE = 0
 P_SIDE = 1
 SIDE_COLS = COLS // 2
@@ -110,23 +110,23 @@ def tile_tverskylayer_pa_k_kernel(
             nc.sync.dma_start(out=x_blk[b][:], in_=x_rows[:, :, first_k : first_k + K_PASS * BLOCK_SIZES[b]])
 
         load_x(0)
+        load_x(1)
         for b in range(BLOCKS):
             first, size = BLOCK_STARTS[b], BLOCK_SIZES[b]
-            if b == 0:
-                load_feature_scales(0)
             nc.sync.dma_start(
                 out=mov_blk[b][:, :, BATCH:COLS].bitcast(I32), in_=p_words[:, first : first + size, :]
             )
+            if b == 0:
+                load_feature_scales(0)
             for g in range(first, first + size):
                 nc.sync.dma_start(out=feat_early[g][:].bitcast(I32), in_=f_words[:, g, 0:EARLY_COLS])
                 if g == first:
                     if b == 0:
                         load_prototype_scales()
-                    if b + 1 < BLOCKS:
+                    elif b + 1 < BLOCKS:
                         load_x(b + 1)
-            if b == 1:
-                for j in range(1, QUADS):
-                    load_feature_scales(j)
+                    if b + 2 < BLOCKS and BLOCK_STARTS[b + 2] % PLANES == 0:
+                        load_feature_scales(BLOCK_STARTS[b + 2] // PLANES)
         for j in range(QUADS):
             nc.sync.dma_start(
                 out=feat_late[j][:].bitcast(I32),
@@ -260,17 +260,17 @@ def tile_tverskylayer_pa_k_kernel(
 
         accs = [psum_early.tile([P, COLS], F32, name="acc%d" % m, tag="early") for m in range(EARLY_TILES)]
         banks = transpose_block(0, sort_block(0))
-        quantise_block(0, banks)
         sorted_words = sort_block(1)
+        quantise_block(0, banks)
         for b in range(BLOCKS - 1):
             passes = [(g, m) for g in range(BLOCK_STARTS[b], BLOCK_STARTS[b + 1]) for m in range(EARLY_TILES)]
-            for g, m in passes[:PASSES_BEFORE_TRANSPOSES]:
+            for g, m in passes[: PASSES_BEFORE_TRANSPOSES[b]]:
                 first_stage_pass(accs[m][:], g, m, slice(0, COLS))
             banks = transpose_block(b + 1, sorted_words)
             quantise_block(b + 1, banks)
             if b + 2 < BLOCKS:
                 sorted_words = sort_block(b + 2)
-            for g, m in passes[PASSES_BEFORE_TRANSPOSES:]:
+            for g, m in passes[PASSES_BEFORE_TRANSPOSES[b] :]:
                 first_stage_pass(accs[m][:], g, m, slice(0, COLS))
         for m in range(EARLY_TILES):
             for g in range(BLOCK_STARTS[BLOCKS - 1], GROUPS):

@@ -87,6 +87,16 @@ def tile_tverskylayer_pa_k_kernel(
         ident = keep.tile([P, P], F32, name="ident")
         make_identity(nc, ident[:])
 
+        idle_operand = keep.tile([P, COLS], BF16, name="idle_operand")
+        nc.vector.memset(idle_operand[:], 0.0)
+        idle_result = psum_early.tile([P, COLS], F32, name="idle_result", tag="early")
+
+        def idle_products(count):
+            for product in range(count):
+                nc.tensor.matmul(
+                    out=idle_result[:], lhsT=idle_operand[:, 0:P], rhs=idle_operand[:], start=True, stop=True
+                )
+
         nc.vector.memset(feat_planes[:, 0, :].bitcast(I32), 0)
         nc.vector.memset(mov_planes[:, :, BATCH:COLS].bitcast(I32), 0)
         nc.gpsimd.memset(feat_planes[:, 1:QUADS, :].bitcast(I32), 0)
@@ -258,10 +268,11 @@ def tile_tverskylayer_pa_k_kernel(
             second_stage_pass(xd[r], h, SQUARE_X + P * r, REST_P)
             second_stage_pass(common[r], h, SQUARE_X + P * r, SQUARE_P)
 
-        accs = [psum_early.tile([P, COLS], F32, name="acc%d" % m, tag="early") for m in range(EARLY_TILES)]
+        idle_products(4)
         banks = transpose_block(0, sort_block(0))
         sorted_words = sort_block(1)
         quantise_block(0, banks)
+        accs = [psum_early.tile([P, COLS], F32, name="acc%d" % m, tag="early") for m in range(EARLY_TILES)]
         for b in range(BLOCKS - 1):
             passes = [(g, m) for g in range(BLOCK_STARTS[b], BLOCK_STARTS[b + 1]) for m in range(EARLY_TILES)]
             for g, m in passes[: PASSES_BEFORE_TRANSPOSES[b]]:
@@ -270,6 +281,8 @@ def tile_tverskylayer_pa_k_kernel(
             quantise_block(b + 1, banks)
             if b + 2 < BLOCKS:
                 sorted_words = sort_block(b + 2)
+            if b == 0:
+                idle_products(4)
             for g, m in passes[PASSES_BEFORE_TRANSPOSES[b] :]:
                 first_stage_pass(accs[m][:], g, m, slice(0, COLS))
         for m in range(EARLY_TILES):
@@ -314,7 +327,6 @@ def tile_tverskylayer_pa_k_kernel(
         common = [psum_early.tile([P, SLOT], F32, name="common%d" % r, tag="early") for r in range(ROW_TILES)]
         for r in range(ROW_TILES):
             second_stage(0, r)
-        for r in range(ROW_TILES):
             second_stage(1, r)
             part = stage.tile([P, PROTOS], F32, name="part")
             nc.scalar.activation(out=part[:], in_=pd[r][:], func=ACT.Copy, scale=weights[:, 2:3])

@@ -35,6 +35,7 @@ EARLY_COLS = EARLY_TILES * P
 BLOCK_SIZES = [1, 1] + 7 * [2]
 BLOCK_STARTS = [sum(BLOCK_SIZES[:b]) for b in range(len(BLOCK_SIZES))]
 BLOCKS = len(BLOCK_SIZES)
+PLANE_RANGES = [(0, 4), (4, GROUPS)]
 PLANES = 4
 QUADS = GROUPS // PLANES
 PASSES_BEFORE_TRANSPOSES = [0] + 8 * [3]
@@ -77,7 +78,10 @@ def tile_tverskylayer_pa_k_kernel(
         mov_blk = [
             keep.tile([P, size, COLS], U32, name="mov%d" % b, align_bytes=64) for b, size in enumerate(BLOCK_SIZES)
         ]
-        mov_planes = keep.tile([P, GROUPS, COLS], U8, name="mov_planes", align_bytes=64)
+        mov_planes = [
+            keep.tile([P, stop - first, COLS], U8, name="mov_planes%d" % first, align_bytes=64)
+            for first, stop in PLANE_RANGES
+        ]
         feat_early = [keep.tile([P, EARLY_COLS], U32, name="fe%d" % g, align_bytes=64) for g in range(GROUPS)]
         feat_late = [
             keep.tile([P, PLANES, LATE_TILES * P], U32, name="fl%d" % j, align_bytes=64) for j in range(QUADS)
@@ -87,8 +91,11 @@ def tile_tverskylayer_pa_k_kernel(
         ident = keep.tile([P, P], F32, name="ident")
         make_identity(nc, ident[:])
 
+        nc.vector.memset(feat_planes[:, 0, :].bitcast(I32), 0)
+        nc.gpsimd.memset(feat_planes[:, 1:QUADS, :].bitcast(I32), 0)
+
         idle_operand = keep.tile([P, COLS], BF16, name="idle_operand")
-        nc.vector.memset(idle_operand[:], 0.0)
+        nc.vector.memset(idle_operand[:].bitcast(I32), 0)
         idle_result = psum_early.tile([P, COLS], F32, name="idle_result", tag="early")
 
         def idle_products(count):
@@ -97,9 +104,8 @@ def tile_tverskylayer_pa_k_kernel(
                     out=idle_result[:], lhsT=idle_operand[:, 0:P], rhs=idle_operand[:], start=True, stop=True
                 )
 
-        nc.vector.memset(feat_planes[:, 0, :].bitcast(I32), 0)
-        nc.vector.memset(mov_planes[:, :, BATCH:COLS].bitcast(I32), 0)
-        nc.gpsimd.memset(feat_planes[:, 1:QUADS, :].bitcast(I32), 0)
+        nc.vector.memset(mov_planes[0][:, :, BATCH:COLS].bitcast(I32), 0)
+        nc.gpsimd.memset(mov_planes[1][:, :, BATCH:COLS].bitcast(I32), 0)
 
         def load_feature_scales(j):
             for quadrant in range(4):
@@ -108,11 +114,12 @@ def tile_tverskylayer_pa_k_kernel(
                     in_=f_scales[PLANES * j : PLANES * (j + 1), 4 * quadrant : 4 * quadrant + 4, :],
                 )
 
-        def load_prototype_scales():
+        def load_prototype_scales(part):
+            first, stop = PLANE_RANGES[part]
             for r in range(4):
                 nc.sync.dma_start(
-                    out=mov_planes[r:P:32, :, BATCH:COLS].bitcast(I32),
-                    in_=p_scales[:, r:16:4, :].rearrange("g q n -> q g n"),
+                    out=mov_planes[part][r:P:32, :, BATCH:COLS].bitcast(I32),
+                    in_=p_scales[first:stop, r:16:4, :].rearrange("g q n -> q g n"),
                 )
 
         def load_x(b):
@@ -120,23 +127,27 @@ def tile_tverskylayer_pa_k_kernel(
             nc.sync.dma_start(out=x_blk[b][:], in_=x_rows[:, :, first_k : first_k + K_PASS * BLOCK_SIZES[b]])
 
         load_x(0)
+        load_feature_scales(0)
         load_x(1)
         for b in range(BLOCKS):
             first, size = BLOCK_STARTS[b], BLOCK_SIZES[b]
             nc.sync.dma_start(
                 out=mov_blk[b][:, :, BATCH:COLS].bitcast(I32), in_=p_words[:, first : first + size, :]
             )
-            if b == 0:
-                load_feature_scales(0)
             for g in range(first, first + size):
-                nc.sync.dma_start(out=feat_early[g][:].bitcast(I32), in_=f_words[:, g, 0:EARLY_COLS])
+                parts = 2 if g == 0 else 1
+                for part in range(parts):
+                    cols = slice(EARLY_COLS // parts * part, EARLY_COLS // parts * (part + 1))
+                    nc.sync.dma_start(out=feat_early[g][:, cols].bitcast(I32), in_=f_words[:, g, cols])
+                    if g == part == 0:
+                        load_prototype_scales(0)
                 if g == first:
-                    if b == 0:
-                        load_prototype_scales()
-                    elif b + 1 < BLOCKS:
+                    if 0 < b < BLOCKS - 1:
                         load_x(b + 1)
                     if b + 2 < BLOCKS and BLOCK_STARTS[b + 2] % PLANES == 0:
                         load_feature_scales(BLOCK_STARTS[b + 2] // PLANES)
+                    if b + 1 < BLOCKS and BLOCK_STARTS[b + 1] == PLANE_RANGES[1][0]:
+                        load_prototype_scales(1)
         for j in range(QUADS):
             nc.sync.dma_start(
                 out=feat_late[j][:].bitcast(I32),
@@ -149,6 +160,10 @@ def tile_tverskylayer_pa_k_kernel(
         nc.sync.dma_start(out=alpha_bf[:], in_=alpha.partition_broadcast(P))
         nc.sync.dma_start(out=beta_bf[:], in_=beta.partition_broadcast(P))
 
+        def mov_plane(g, cols):
+            part = 0 if g < PLANE_RANGES[0][1] else 1
+            return mov_planes[part][:, g - PLANE_RANGES[part][0], cols]
+
         def sort_block(b):
             size = BLOCK_SIZES[b]
             sorted_words = stage.tile([P, ROW_TILES * size, 2, P], F32, name="sorted_words")
@@ -156,7 +171,11 @@ def tile_tverskylayer_pa_k_kernel(
                 out=sorted_words[:],
                 in_=x_blk[b][:].rearrange("p r k -> p (r k)").bitcast(F32).rearrange("p (i w u) -> p i u w", w=P, u=2),
             )
-            return sorted_words
+            return sorted_words[:].rearrange("p (r i) u w -> p r i u w", r=ROW_TILES)
+
+        def unsorted_block(b):
+            words = x_blk[b][:].bitcast(F32)
+            return words.rearrange("p r (i w u) -> p r i u w", w=P, u=2)
 
         def transpose_block(b, sorted_words):
             banks = []
@@ -165,7 +184,7 @@ def tile_tverskylayer_pa_k_kernel(
                 for r in range(ROW_TILES):
                     for u in range(2):
                         nc.tensor.transpose(
-                            xt[:, u, P * r : P * (r + 1)], sorted_words[:, BLOCK_SIZES[b] * r + i, u, :], ident[:]
+                            xt[:, u, P * r : P * (r + 1)], sorted_words[:, r, i, u, :], ident[:]
                         )
                 banks.append(xt)
             return banks
@@ -180,7 +199,7 @@ def tile_tverskylayer_pa_k_kernel(
                 )
                 nc.vector.quantize_mx(
                     out=mov_blk[b][:, i, 0:BATCH].bitcast(FP8X4),
-                    scales=mov_planes[:, BLOCK_STARTS[b] + i, 0:BATCH],
+                    scales=mov_plane(BLOCK_STARTS[b] + i, slice(0, BATCH)),
                     in_=grouped[:].rearrange("p c t -> p (c t)"),
                 )
 
@@ -199,7 +218,7 @@ def tile_tverskylayer_pa_k_kernel(
                 lhsT=words.bitcast(FP8X4),
                 lhsT_scale=feat_planes[first_row:P, g // PLANES, P * m : P * (m + 1)],
                 rhs=mov_blk[b][:, g - BLOCK_STARTS[b], cols].bitcast(FP8X4),
-                rhs_scale=mov_planes[:, g, cols],
+                rhs_scale=mov_plane(g, cols),
                 start=(g == 0),
                 stop=(g == GROUPS - 1),
             )
@@ -269,7 +288,7 @@ def tile_tverskylayer_pa_k_kernel(
             second_stage_pass(common[r], h, SQUARE_X + P * r, SQUARE_P)
 
         idle_products(4)
-        banks = transpose_block(0, sort_block(0))
+        banks = transpose_block(0, unsorted_block(0))
         sorted_words = sort_block(1)
         quantise_block(0, banks)
         accs = [psum_early.tile([P, COLS], F32, name="acc%d" % m, tag="early") for m in range(EARLY_TILES)]
@@ -282,7 +301,7 @@ def tile_tverskylayer_pa_k_kernel(
             if b + 2 < BLOCKS:
                 sorted_words = sort_block(b + 2)
             if b == 0:
-                idle_products(4)
+                idle_products(2)
             for g, m in passes[PASSES_BEFORE_TRANSPOSES[b] :]:
                 first_stage_pass(accs[m][:], g, m, slice(0, COLS))
         for m in range(EARLY_TILES):
@@ -320,22 +339,30 @@ def tile_tverskylayer_pa_k_kernel(
             square(1, SQUARE_X, P * r, P, nc.scalar)
             rest(1, REST_X, P * r, P)
             quantise(1, REST_X + P * r, P)
-            quantise(1, SQUARE_X + P * r, P)
+            if r == 0:
+                quantise(1, SQUARE_X, P)
 
         pd = [psum_early.tile([P, SLOT], F32, name="pd%d" % r, tag="early") for r in range(ROW_TILES)]
         xd = [psum_early.tile([P, SLOT], F32, name="xd%d" % r, tag="early") for r in range(ROW_TILES)]
         common = [psum_early.tile([P, SLOT], F32, name="common%d" % r, tag="early") for r in range(ROW_TILES)]
+        parts = [stage.tile([P, PROTOS], F32, name="part%d" % r) for r in range(ROW_TILES)]
+        boths = [stage.tile([P, PROTOS], F32, name="both%d" % r) for r in range(ROW_TILES)]
+        results = [stage.tile([P, PROTOS], F32, name="result%d" % r) for r in range(ROW_TILES)]
+
+        def add_weighted(result, source, weight, addend):
+            nc.vector.scalar_tensor_tensor(
+                out=result[:], in0=source[:], scalar=weights[:, weight : weight + 1], in1=addend[:], op0=ALU.mult, op1=ALU.add
+            )
+
+        second_stage(0, 0)
+        second_stage(1, 0)
+        nc.vector.tensor_scalar(out=parts[0][:], in0=pd[0][:], scalar1=weights[:, 2:3], scalar2=None, op0=ALU.mult)
+        quantise(1, SQUARE_X + P, P)
+        second_stage(0, 1)
+        second_stage(1, 1)
+        nc.scalar.activation(out=parts[1][:], in_=pd[1][:], func=ACT.Copy, scale=weights[:, 2:3])
         for r in range(ROW_TILES):
-            second_stage(0, r)
-            second_stage(1, r)
-            part = stage.tile([P, PROTOS], F32, name="part")
-            nc.scalar.activation(out=part[:], in_=pd[r][:], func=ACT.Copy, scale=weights[:, 2:3])
-            both = stage.tile([P, PROTOS], F32, name="both")
-            nc.vector.scalar_tensor_tensor(
-                out=both[:], in0=xd[r][:], scalar=weights[:, 1:2], in1=part[:], op0=ALU.mult, op1=ALU.add
-            )
-            result = stage.tile([P, PROTOS], F32, name="result")
-            nc.vector.scalar_tensor_tensor(
-                out=result[:], in0=common[r][:], scalar=weights[:, 0:1], in1=both[:], op0=ALU.mult, op1=ALU.add
-            )
-            nc.sync.dma_start(out=out[P * r : P * (r + 1), :], in_=result[:])
+            add_weighted(boths[r], xd[r], 1, parts[r])
+        for r in range(ROW_TILES):
+            add_weighted(results[r], common[r], 0, boths[r])
+            nc.sync.dma_start(out=out[P * r : P * (r + 1), :], in_=results[r][:])

@@ -35,7 +35,7 @@ EARLY_COLS = EARLY_TILES * P
 BLOCK_SIZES = [1, 1] + 7 * [2]
 BLOCK_STARTS = [sum(BLOCK_SIZES[:b]) for b in range(len(BLOCK_SIZES))]
 BLOCKS = len(BLOCK_SIZES)
-PLANE_RANGES = [(0, 4), (4, GROUPS)]
+PLANE_RANGES = [(0, 8), (8, GROUPS)]
 PLANES = 4
 QUADS = GROUPS // PLANES
 PASSES_BEFORE_TRANSPOSES = [0] + 8 * [3]
@@ -69,8 +69,6 @@ def tile_tverskylayer_pa_k_kernel(
         x_rows = x.rearrange("(r p) k -> p r k", p=P)
         f_words = features_words.rearrange("g p n t -> p g (n t)").bitcast(I32)
         p_words = prototypes_words.rearrange("g p n t -> p g (n t)").bitcast(I32)
-        f_scales = features_scales.bitcast(I32)
-        p_scales = prototypes_scales.bitcast(I32)
 
         x_blk = [
             keep.tile([P, ROW_TILES, size * K_PASS], BF16, name="x%d" % b) for b, size in enumerate(BLOCK_SIZES)
@@ -107,27 +105,31 @@ def tile_tverskylayer_pa_k_kernel(
         nc.vector.memset(mov_planes[0][:, :, BATCH:COLS].bitcast(I32), 0)
         nc.gpsimd.memset(mov_planes[1][:, :, BATCH:COLS].bitcast(I32), 0)
 
-        def load_feature_scales(j):
+        def load_feature_scales(engine, word, j):
             for quadrant in range(4):
-                nc.sync.dma_start(
-                    out=feat_planes[32 * quadrant : 32 * quadrant + 16, j, :].bitcast(I32),
-                    in_=f_scales[PLANES * j : PLANES * (j + 1), 4 * quadrant : 4 * quadrant + 4, :],
+                engine.dma_start(
+                    out=feat_planes[32 * quadrant : 32 * quadrant + 16, j, :].bitcast(word),
+                    in_=features_scales[PLANES * j : PLANES * (j + 1), 4 * quadrant : 4 * quadrant + 4, :].bitcast(word),
                 )
 
-        def load_prototype_scales(part):
+        def load_prototype_scales(engine, word, part):
             first, stop = PLANE_RANGES[part]
             for r in range(4):
-                nc.sync.dma_start(
-                    out=mov_planes[part][r:P:32, :, BATCH:COLS].bitcast(I32),
-                    in_=p_scales[first:stop, r:16:4, :].rearrange("g q n -> q g n"),
+                engine.dma_start(
+                    out=mov_planes[part][r:P:32, :, BATCH:COLS].bitcast(word),
+                    in_=prototypes_scales.bitcast(word)[first:stop, r:16:4, :].rearrange("g q n -> q g n"),
                 )
+
+        load_feature_scales(nc.gpsimd, F32, 2)
+        load_prototype_scales(nc.gpsimd, F32, 1)
+        load_feature_scales(nc.gpsimd, F32, 3)
 
         def load_x(b):
             first_k = K_PASS * BLOCK_STARTS[b]
             nc.sync.dma_start(out=x_blk[b][:], in_=x_rows[:, :, first_k : first_k + K_PASS * BLOCK_SIZES[b]])
 
         load_x(0)
-        load_feature_scales(0)
+        load_feature_scales(nc.sync, I32, 0)
         load_x(1)
         for b in range(BLOCKS):
             first, size = BLOCK_STARTS[b], BLOCK_SIZES[b]
@@ -140,14 +142,11 @@ def tile_tverskylayer_pa_k_kernel(
                     cols = slice(EARLY_COLS // parts * part, EARLY_COLS // parts * (part + 1))
                     nc.sync.dma_start(out=feat_early[g][:, cols].bitcast(I32), in_=f_words[:, g, cols])
                     if g == part == 0:
-                        load_prototype_scales(0)
-                if g == first:
-                    if 0 < b < BLOCKS - 1:
-                        load_x(b + 1)
-                    if b + 2 < BLOCKS and BLOCK_STARTS[b + 2] % PLANES == 0:
-                        load_feature_scales(BLOCK_STARTS[b + 2] // PLANES)
-                    if b + 1 < BLOCKS and BLOCK_STARTS[b + 1] == PLANE_RANGES[1][0]:
-                        load_prototype_scales(1)
+                        load_prototype_scales(nc.sync, I32, 0)
+                if g == first and 0 < b < BLOCKS - 1:
+                    load_x(b + 1)
+                if g == 1:
+                    load_feature_scales(nc.sync, I32, 1)
         for j in range(QUADS):
             nc.sync.dma_start(
                 out=feat_late[j][:].bitcast(I32),

@@ -74,17 +74,17 @@ def tile_tverskylayer_pa_k_kernel(
             keep.tile([P, ROW_TILES, size * K_PASS], BF16, name="x%d" % b) for b, size in enumerate(BLOCK_SIZES)
         ]
         mov_blk = [
-            keep.tile([P, size, COLS], U32, name="mov%d" % b, align_bytes=64) for b, size in enumerate(BLOCK_SIZES)
+            keep.tile([P, size, COLS], U32, name="mov%d" % b, align_bytes=256) for b, size in enumerate(BLOCK_SIZES)
         ]
         mov_planes = [
-            keep.tile([P, stop - first, COLS], U8, name="mov_planes%d" % first, align_bytes=64)
+            keep.tile([P, stop - first, COLS], U8, name="mov_planes%d" % first, align_bytes=256)
             for first, stop in PLANE_RANGES
         ]
-        feat_early = [keep.tile([P, EARLY_COLS], U32, name="fe%d" % g, align_bytes=64) for g in range(GROUPS)]
+        feat_early = [keep.tile([P, EARLY_COLS], U32, name="fe%d" % g, align_bytes=256) for g in range(GROUPS)]
         feat_late = [
-            keep.tile([P, PLANES, LATE_TILES * P], U32, name="fl%d" % j, align_bytes=64) for j in range(QUADS)
+            keep.tile([P, PLANES, LATE_TILES * P], U32, name="fl%d" % j, align_bytes=256) for j in range(QUADS)
         ]
-        feat_planes = keep.tile([P, QUADS, FEATURES], U8, name="feat_planes", align_bytes=64)
+        feat_planes = keep.tile([P, QUADS, FEATURES], U8, name="feat_planes", align_bytes=256)
 
         ident = keep.tile([P, P], F32, name="ident")
         make_identity(nc, ident[:])
@@ -190,7 +190,7 @@ def tile_tverskylayer_pa_k_kernel(
 
         def quantise_block(b, banks):
             for i in range(BLOCK_SIZES[b]):
-                grouped = stage.tile([P, BATCH, PACK], BF16, name="grouped", align_bytes=64)
+                grouped = stage.tile([P, BATCH, PACK], BF16, name="grouped", align_bytes=256)
                 pairs = grouped[:].rearrange("p c t -> p (c t)").bitcast(F32)
                 nc.scalar.copy(
                     out=pairs.rearrange("p (c u) -> p c u", u=2),
@@ -226,14 +226,14 @@ def tile_tverskylayer_pa_k_kernel(
         SLOT = SIDE_COLS
         REST_X, SQUARE_X, SQUARE_P, REST_P = 0, SLOT, 2 * SLOT, 3 * SLOT
         s2_values = [
-            keep.tile([P, 4 * SLOT, PACK], BF16, name="s2_values%d" % h, align_bytes=64)
+            keep.tile([P, 4 * SLOT, PACK], BF16, name="s2_values%d" % h, align_bytes=256)
             for h in range(HALVES)
         ]
         s2_words = [
-            keep.tile([P, 4 * SLOT], U32, name="s2_words%d" % h, align_bytes=64) for h in range(HALVES)
+            keep.tile([P, 4 * SLOT], U32, name="s2_words%d" % h, align_bytes=256) for h in range(HALVES)
         ]
         s2_planes = [
-            keep.tile([P, 4 * SLOT], U8, name="s2_planes%d" % h, align_bytes=64) for h in range(HALVES)
+            keep.tile([P, 4 * SLOT], U8, name="s2_planes%d" % h, align_bytes=256) for h in range(HALVES)
         ]
 
         def relu(sums, m, cols):
@@ -344,9 +344,9 @@ def tile_tverskylayer_pa_k_kernel(
         pd = [psum_early.tile([P, SLOT], F32, name="pd%d" % r, tag="early") for r in range(ROW_TILES)]
         xd = [psum_early.tile([P, SLOT], F32, name="xd%d" % r, tag="early") for r in range(ROW_TILES)]
         common = [psum_early.tile([P, SLOT], F32, name="common%d" % r, tag="early") for r in range(ROW_TILES)]
-        parts = [stage.tile([P, PROTOS], F32, name="part%d" % r) for r in range(ROW_TILES)]
-        boths = [stage.tile([P, PROTOS], F32, name="both%d" % r) for r in range(ROW_TILES)]
-        results = [stage.tile([P, PROTOS], F32, name="result%d" % r) for r in range(ROW_TILES)]
+        parts = [keep.tile([P, PROTOS], F32, name="part%d" % r) for r in range(ROW_TILES)]
+        boths = [keep.tile([P, PROTOS], F32, name="both%d" % r) for r in range(ROW_TILES)]
+        results = [keep.tile([P, PROTOS], F32, name="result%d" % r) for r in range(ROW_TILES)]
 
         def add_weighted(result, source, weight, addend):
             nc.vector.scalar_tensor_tensor(

@@ -71,7 +71,7 @@ def tile_tverskylayer_pa_k_kernel(
         p_words = prototypes_words.rearrange("g p n t -> p g (n t)").bitcast(I32)
 
         x_blk = [
-            keep.tile([P, ROW_TILES, size * K_PASS], BF16, name="x%d" % b) for b, size in enumerate(BLOCK_SIZES)
+            keep.tile([P, ROW_TILES, size * K_PASS], BF16, name="x%d" % b, align_bytes=256) for b, size in enumerate(BLOCK_SIZES)
         ]
         mov_blk = [
             keep.tile([P, size, COLS], U32, name="mov%d" % b, align_bytes=256) for b, size in enumerate(BLOCK_SIZES)
@@ -86,13 +86,13 @@ def tile_tverskylayer_pa_k_kernel(
         ]
         feat_planes = keep.tile([P, QUADS, FEATURES], U8, name="feat_planes", align_bytes=256)
 
-        ident = keep.tile([P, P], F32, name="ident")
+        ident = keep.tile([P, P], F32, name="ident", align_bytes=256)
         make_identity(nc, ident[:])
 
         nc.vector.memset(feat_planes[:, 0, :].bitcast(I32), 0)
         nc.gpsimd.memset(feat_planes[:, 1:QUADS, :].bitcast(I32), 0)
 
-        idle_operand = keep.tile([P, COLS], BF16, name="idle_operand")
+        idle_operand = keep.tile([P, COLS], BF16, name="idle_operand", align_bytes=256)
         nc.vector.memset(idle_operand[:].bitcast(I32), 0)
         idle_result = psum_early.tile([P, COLS], F32, name="idle_result", tag="early")
 
@@ -165,7 +165,7 @@ def tile_tverskylayer_pa_k_kernel(
 
         def sort_block(b):
             size = BLOCK_SIZES[b]
-            sorted_words = stage.tile([P, ROW_TILES * size, 2, P], F32, name="sorted_words")
+            sorted_words = stage.tile([P, ROW_TILES * size, 2, P], F32, name="sorted_words", align_bytes=256)
             nc.vector.tensor_copy(
                 out=sorted_words[:],
                 in_=x_blk[b][:].rearrange("p r k -> p (r k)").bitcast(F32).rearrange("p (i w u) -> p i u w", w=P, u=2),
@@ -222,7 +222,7 @@ def tile_tverskylayer_pa_k_kernel(
                 stop=(g == GROUPS - 1),
             )
 
-        pres = [keep.tile([P, HALF_TILES, COLS], F32, name="pres%d" % h) for h in range(HALVES)]
+        pres = [keep.tile([P, HALF_TILES, COLS], F32, name="pres%d" % h, align_bytes=256) for h in range(HALVES)]
         SLOT = SIDE_COLS
         REST_X, SQUARE_X, SQUARE_P, REST_P = 0, SLOT, 2 * SLOT, 3 * SLOT
         s2_values = [
@@ -344,9 +344,9 @@ def tile_tverskylayer_pa_k_kernel(
         pd = [psum_early.tile([P, SLOT], F32, name="pd%d" % r, tag="early") for r in range(ROW_TILES)]
         xd = [psum_early.tile([P, SLOT], F32, name="xd%d" % r, tag="early") for r in range(ROW_TILES)]
         common = [psum_early.tile([P, SLOT], F32, name="common%d" % r, tag="early") for r in range(ROW_TILES)]
-        parts = [keep.tile([P, PROTOS], F32, name="part%d" % r) for r in range(ROW_TILES)]
-        boths = [keep.tile([P, PROTOS], F32, name="both%d" % r) for r in range(ROW_TILES)]
-        results = [keep.tile([P, PROTOS], F32, name="result%d" % r) for r in range(ROW_TILES)]
+        parts = [keep.tile([P, PROTOS], F32, name="part%d" % r, align_bytes=256) for r in range(ROW_TILES)]
+        boths = [keep.tile([P, PROTOS], F32, name="both%d" % r, align_bytes=256) for r in range(ROW_TILES)]
+        results = [keep.tile([P, PROTOS], F32, name="result%d" % r, align_bytes=256) for r in range(ROW_TILES)]
 
         def add_weighted(result, source, weight, addend):
             nc.vector.scalar_tensor_tensor(

from contextlib import ExitStack

import concourse.mybir as mybir
from concourse.masks import make_identity

F32 = mybir.dt.float32
BF16 = mybir.dt.bfloat16
I32 = mybir.dt.int32
U32 = mybir.dt.uint32
U8 = mybir.dt.uint8
FP8X4 = mybir.dt.float8_e4m3fn_x4
ACT = mybir.ActivationFunctionType
ALU = mybir.AluOpType

P = 128
PACK = 4
K_PASS = P * PACK

BATCH = 256
PROTOS = 256
INPUTS = 8192
FEATURES = 1024

COLS = BATCH + PROTOS
GROUPS = INPUTS // K_PASS
F_TILES = FEATURES // P
HALF_TILES = PACK
HALVES = F_TILES // HALF_TILES
HALF_COLS = HALF_TILES * P
ROW_TILES = BATCH // P

EARLY_TILES = 6
LATE_TILES = F_TILES - EARLY_TILES
EARLY_COLS = EARLY_TILES * P
BLOCK_SIZES = [1, 1] + 7 * [2]
BLOCK_STARTS = [sum(BLOCK_SIZES[:b]) for b in range(len(BLOCK_SIZES))]
BLOCKS = len(BLOCK_SIZES)
PLANE_RANGES = [(0, 8), (8, GROUPS)]
PLANES = 4
QUADS = GROUPS // PLANES
PASSES_BEFORE_TRANSPOSES = [0] + 8 * [3]
X_SIDE = 0
P_SIDE = 1
SIDE_COLS = COLS // 2

FLOPS = 2 * COLS * INPUTS * FEATURES + 3 * 2 * BATCH * PROTOS * FEATURES


def tile_tverskylayer_pa_k_kernel(
    tc,
    x,
    features_words,
    features_scales,
    prototypes_words,
    prototypes_scales,
    alpha,
    beta,
    theta,
    out,
):
    nc = tc.nc
    with ExitStack() as ctx:
        ctx.enter_context(tc.manual_schedule())
        keep = ctx.enter_context(tc.tile_pool(name="keep", bufs=1))
        stage = ctx.enter_context(tc.tile_pool(name="stage", bufs=4))
        psum_early = ctx.enter_context(tc.psum_pool(name="psum_early", bufs=EARLY_TILES))
        psum_late = ctx.enter_context(tc.psum_pool(name="psum_late", bufs=LATE_TILES))

        x_rows = x.rearrange("(r p) k -> p r k", p=P)
        f_words = features_words.rearrange("g p n t -> p g (n t)").bitcast(I32)
        p_words = prototypes_words.rearrange("g p n t -> p g (n t)").bitcast(I32)

        x_blk = [
            keep.tile([P, ROW_TILES, size * K_PASS], BF16, name="x%d" % b, align_bytes=256) for b, size in enumerate(BLOCK_SIZES)
        ]
        mov_blk = [
            keep.tile([P, size, COLS], U32, name="mov%d" % b, align_bytes=256) for b, size in enumerate(BLOCK_SIZES)
        ]
        mov_planes = [
            keep.tile([P, stop - first, COLS], U8, name="mov_planes%d" % first, align_bytes=256)
            for first, stop in PLANE_RANGES
        ]
        feat_early = [keep.tile([P, EARLY_COLS], U32, name="fe%d" % g, align_bytes=256) for g in range(GROUPS)]
        feat_late = [
            keep.tile([P, PLANES, LATE_TILES * P], U32, name="fl%d" % j, align_bytes=256) for j in range(QUADS)
        ]
        feat_planes = keep.tile([P, QUADS, FEATURES], U8, name="feat_planes", align_bytes=256)

        ident = keep.tile([P, P], F32, name="ident", align_bytes=256)
        make_identity(nc, ident[:])

        nc.vector.memset(feat_planes[:, 0, :].bitcast(I32), 0)
        nc.gpsimd.memset(feat_planes[:, 1:QUADS, :].bitcast(I32), 0)

        idle_operand = keep.tile([P, COLS], BF16, name="idle_operand", align_bytes=256)
        nc.vector.memset(idle_operand[:].bitcast(I32), 0)
        idle_result = psum_early.tile([P, COLS], F32, name="idle_result", tag="early")

        def idle_products(count):
            for product in range(count):
                nc.tensor.matmul(
                    out=idle_result[:], lhsT=idle_operand[:, 0:P], rhs=idle_operand[:], start=True, stop=True
                )

        nc.vector.memset(mov_planes[0][:, :, BATCH:COLS].bitcast(I32), 0)
        nc.gpsimd.memset(mov_planes[1][:, :, BATCH:COLS].bitcast(I32), 0)

        def load_feature_scales(engine, word, j):
            for quadrant in range(4):
                engine.dma_start(
                    out=feat_planes[32 * quadrant : 32 * quadrant + 16, j, :].bitcast(word),
                    in_=features_scales[PLANES * j : PLANES * (j + 1), 4 * quadrant : 4 * quadrant + 4, :].bitcast(word),
                )

        def load_prototype_scales(engine, word, part):
            first, stop = PLANE_RANGES[part]
            for r in range(4):
                engine.dma_start(
                    out=mov_planes[part][r:P:32, :, BATCH:COLS].bitcast(word),
                    in_=prototypes_scales.bitcast(word)[first:stop, r:16:4, :].rearrange("g q n -> q g n"),
                )

        load_feature_scales(nc.gpsimd, F32, 2)
        load_prototype_scales(nc.gpsimd, F32, 1)
        load_feature_scales(nc.gpsimd, F32, 3)

        def load_x(b):
            first_k = K_PASS * BLOCK_STARTS[b]
            nc.sync.dma_start(out=x_blk[b][:], in_=x_rows[:, :, first_k : first_k + K_PASS * BLOCK_SIZES[b]])

        load_x(0)
        load_feature_scales(nc.sync, I32, 0)
        load_x(1)
        for b in range(BLOCKS):
            first, size = BLOCK_STARTS[b], BLOCK_SIZES[b]
            nc.sync.dma_start(
                out=mov_blk[b][:, :, BATCH:COLS].bitcast(I32), in_=p_words[:, first : first + size, :]
            )
            for g in range(first, first + size):
                parts = 2 if g == 0 else 1
                for part in range(parts):
                    cols = slice(EARLY_COLS // parts * part, EARLY_COLS // parts * (part + 1))
                    nc.sync.dma_start(out=feat_early[g][:, cols].bitcast(I32), in_=f_words[:, g, cols])
                    if g == part == 0:
                        load_prototype_scales(nc.sync, I32, 0)
                if g == first and 0 < b < BLOCKS - 1:
                    load_x(b + 1)
                if g == 1:
                    load_feature_scales(nc.sync, I32, 1)
        for j in range(QUADS):
            nc.sync.dma_start(
                out=feat_late[j][:].bitcast(I32),
                in_=f_words[:, PLANES * j : PLANES * (j + 1), EARLY_COLS:FEATURES],
            )
        theta_bf = keep.tile([P, 1], BF16, name="theta_bf")
        alpha_bf = keep.tile([P, 1], BF16, name="alpha_bf")
        beta_bf = keep.tile([P, 1], BF16, name="beta_bf")
        nc.sync.dma_start(out=theta_bf[:], in_=theta.partition_broadcast(P))
        nc.sync.dma_start(out=alpha_bf[:], in_=alpha.partition_broadcast(P))
        nc.sync.dma_start(out=beta_bf[:], in_=beta.partition_broadcast(P))

        def mov_plane(g, cols):
            part = 0 if g < PLANE_RANGES[0][1] else 1
            return mov_planes[part][:, g - PLANE_RANGES[part][0], cols]

        def sort_block(b):
            size = BLOCK_SIZES[b]
            sorted_words = stage.tile([P, ROW_TILES * size, 2, P], F32, name="sorted_words", align_bytes=256)
            nc.vector.tensor_copy(
                out=sorted_words[:],
                in_=x_blk[b][:].rearrange("p r k -> p (r k)").bitcast(F32).rearrange("p (i w u) -> p i u w", w=P, u=2),
            )
            return sorted_words[:].rearrange("p (r i) u w -> p r i u w", r=ROW_TILES)

        def unsorted_block(b):
            words = x_blk[b][:].bitcast(F32)
            return words.rearrange("p r (i w u) -> p r i u w", w=P, u=2)

        def transpose_block(b, sorted_words):
            banks = []
            for i in range(BLOCK_SIZES[b]):
                xt = psum_late.tile([P, 2, BATCH], F32, name="xt", tag="late")
                for r in range(ROW_TILES):
                    for u in range(2):
                        nc.tensor.transpose(
                            xt[:, u, P * r : P * (r + 1)], sorted_words[:, r, i, u, :], ident[:]
                        )
                banks.append(xt)
            return banks

        def quantise_block(b, banks):
            for i in range(BLOCK_SIZES[b]):
                grouped = stage.tile([P, BATCH, PACK], BF16, name="grouped", align_bytes=256)
                pairs = grouped[:].rearrange("p c t -> p (c t)").bitcast(F32)
                nc.scalar.copy(
                    out=pairs.rearrange("p (c u) -> p c u", u=2),
                    in_=banks[i][:].rearrange("p u c -> p c u"),
                )
                nc.vector.quantize_mx(
                    out=mov_blk[b][:, i, 0:BATCH].bitcast(FP8X4),
                    scales=mov_plane(BLOCK_STARTS[b] + i, slice(0, BATCH)),
                    in_=grouped[:].rearrange("p c t -> p (c t)"),
                )

        def block_of(g):
            return max(b for b in range(BLOCKS) if BLOCK_STARTS[b] <= g)

        def first_stage_pass(acc, g, m, cols):
            b = block_of(g)
            first_row = PACK * (g % PLANES)
            if m < EARLY_TILES:
                words = feat_early[g][:, P * m : P * (m + 1)]
            else:
                words = feat_late[g // PLANES][:, g % PLANES, P * (m - EARLY_TILES) : P * (m - EARLY_TILES + 1)]
            nc.tensor.matmul_mx(
                out=acc,
                lhsT=words.bitcast(FP8X4),
                lhsT_scale=feat_planes[first_row:P, g // PLANES, P * m : P * (m + 1)],
                rhs=mov_blk[b][:, g - BLOCK_STARTS[b], cols].bitcast(FP8X4),
                rhs_scale=mov_plane(g, cols),
                start=(g == 0),
                stop=(g == GROUPS - 1),
            )

        pres = [keep.tile([P, HALF_TILES, COLS], F32, name="pres%d" % h, align_bytes=256) for h in range(HALVES)]
        SLOT = SIDE_COLS
        REST_X, SQUARE_X, SQUARE_P, REST_P = 0, SLOT, 2 * SLOT, 3 * SLOT
        s2_values = [
            keep.tile([P, 4 * SLOT, PACK], BF16, name="s2_values%d" % h, align_bytes=256)
            for h in range(HALVES)
        ]
        s2_words = [
            keep.tile([P, 4 * SLOT], U32, name="s2_words%d" % h, align_bytes=256) for h in range(HALVES)
        ]
        s2_planes = [
            keep.tile([P, 4 * SLOT], U8, name="s2_planes%d" % h, align_bytes=256) for h in range(HALVES)
        ]

        def relu(sums, m, cols):
            nc.scalar.activation(out=pres[m // HALF_TILES][:, m % HALF_TILES, cols], in_=sums, func=ACT.Relu)

        def presences(h, first_col, width):
            return pres[h][:, :, first_col : first_col + width].rearrange("p t c -> p c t")

        def square(h, slot, first_col, width, engine):
            values = s2_values[h][:, slot + first_col % SLOT : slot + first_col % SLOT + width, :]
            source = presences(h, first_col, width)
            if engine is nc.scalar:
                nc.scalar.activation(out=values, in_=source, func=ACT.Square)
            else:
                nc.vector.tensor_tensor(out=values, in0=source, in1=source, op=ALU.mult)

        def rest(h, slot, first_col, width):
            nc.vector.tensor_scalar(
                out=s2_values[h][:, slot + first_col % SLOT : slot + first_col % SLOT + width, :],
                in0=presences(h, first_col, width),
                scalar1=-1.0,
                scalar2=1.0,
                op0=ALU.mult,
                op1=ALU.add,
            )

        def quantise(h, first_col, width):
            cols = slice(first_col, first_col + width)
            nc.vector.quantize_mx(
                out=s2_words[h][:, cols].bitcast(FP8X4),
                scales=s2_planes[h][:, cols],
                in_=s2_values[h][:, cols, :].rearrange("p c t -> p (c t)"),
            )

        def second_stage_pass(result, h, stationary_col, moving_col):
            stationary_cols = slice(stationary_col, stationary_col + P)
            moving_cols = slice(moving_col, moving_col + SLOT)
            nc.tensor.matmul_mx(
                out=result[:],
                lhsT=s2_words[h][:, stationary_cols].bitcast(FP8X4),
                lhsT_scale=s2_planes[h][:, stationary_cols],
                rhs=s2_words[h][:, moving_cols].bitcast(FP8X4),
                rhs_scale=s2_planes[h][:, moving_cols],
                start=(h == 0),
                stop=(h == HALVES - 1),
            )

        def second_stage(h, r):
            second_stage_pass(pd[r], h, REST_X + P * r, SQUARE_P)
            second_stage_pass(xd[r], h, SQUARE_X + P * r, REST_P)
            second_stage_pass(common[r], h, SQUARE_X + P * r, SQUARE_P)

        idle_products(4)
        banks = transpose_block(0, unsorted_block(0))
        sorted_words = sort_block(1)
        quantise_block(0, banks)
        accs = [psum_early.tile([P, COLS], F32, name="acc%d" % m, tag="early") for m in range(EARLY_TILES)]
        for b in range(BLOCKS - 1):
            passes = [(g, m) for g in range(BLOCK_STARTS[b], BLOCK_STARTS[b + 1]) for m in range(EARLY_TILES)]
            for g, m in passes[: PASSES_BEFORE_TRANSPOSES[b]]:
                first_stage_pass(accs[m][:], g, m, slice(0, COLS))
            banks = transpose_block(b + 1, sorted_words)
            quantise_block(b + 1, banks)
            if b + 2 < BLOCKS:
                sorted_words = sort_block(b + 2)
            if b == 0:
                idle_products(2)
            for g, m in passes[PASSES_BEFORE_TRANSPOSES[b] :]:
                first_stage_pass(accs[m][:], g, m, slice(0, COLS))
        for m in range(EARLY_TILES):
            for g in range(BLOCK_STARTS[BLOCKS - 1], GROUPS):
                first_stage_pass(accs[m][:], g, m, slice(0, COLS))
            relu(accs[m][:], m, slice(0, COLS))

        square(0, SQUARE_X, 0, SLOT, nc.scalar)
        square(0, SQUARE_P, SLOT, SLOT, nc.vector)
        rest(0, REST_P, SLOT, SLOT)
        rest(0, REST_X, 0, SLOT)
        quantise(0, SQUARE_P, 2 * SLOT)
        quantise(0, REST_X, 2 * SLOT)

        weights = keep.tile([P, 3], F32, name="weights")
        nc.vector.tensor_copy(out=weights[:, 0:1], in_=theta_bf[:])
        nc.vector.tensor_scalar(out=weights[:, 1:2], in0=alpha_bf[:], scalar1=-1.0, scalar2=None, op0=ALU.mult)
        nc.vector.tensor_scalar(out=weights[:, 2:3], in0=beta_bf[:], scalar1=-1.0, scalar2=None, op0=ALU.mult)

        def late_passes(m, first_col, width):
            acc = psum_late.tile([P, width], F32, name="acc_late", tag="late")
            for g in range(GROUPS):
                first_stage_pass(acc[:], g, m, slice(first_col, first_col + width))
            relu(acc[:], m, slice(first_col, first_col + width))

        for m in range(EARLY_TILES, F_TILES):
            late_passes(m, SLOT, SLOT)
        square(1, SQUARE_P, SLOT, SLOT, nc.scalar)
        rest(1, REST_P, SLOT, SLOT)
        quantise(1, SQUARE_P, 2 * SLOT)
        for m in range(EARLY_TILES, F_TILES - 1):
            late_passes(m, 0, SLOT)
        for r in range(ROW_TILES):
            late_passes(F_TILES - 1, P * r, P)
            square(1, SQUARE_X, P * r, P, nc.scalar)
            rest(1, REST_X, P * r, P)
            quantise(1, REST_X + P * r, P)
            if r == 0:
                quantise(1, SQUARE_X, P)

        pd = [psum_early.tile([P, SLOT], F32, name="pd%d" % r, tag="early") for r in range(ROW_TILES)]
        xd = [psum_early.tile([P, SLOT], F32, name="xd%d" % r, tag="early") for r in range(ROW_TILES)]
        common = [psum_early.tile([P, SLOT], F32, name="common%d" % r, tag="early") for r in range(ROW_TILES)]
        parts = [keep.tile([P, PROTOS], F32, name="part%d" % r, align_bytes=256) for r in range(ROW_TILES)]
        boths = [keep.tile([P, PROTOS], F32, name="both%d" % r, align_bytes=256) for r in range(ROW_TILES)]
        results = [keep.tile([P, PROTOS], F32, name="result%d" % r, align_bytes=256) for r in range(ROW_TILES)]

        def add_weighted(result, source, weight, addend):
            nc.vector.scalar_tensor_tensor(
                out=result[:], in0=source[:], scalar=weights[:, weight : weight + 1], in1=addend[:], op0=ALU.mult, op1=ALU.add
            )

        second_stage(0, 0)
        second_stage(1, 0)
        nc.vector.tensor_scalar(out=parts[0][:], in0=pd[0][:], scalar1=weights[:, 2:3], scalar2=None, op0=ALU.mult)
        quantise(1, SQUARE_X + P, P)
        second_stage(0, 1)
        second_stage(1, 1)
        nc.scalar.activation(out=parts[1][:], in_=pd[1][:], func=ACT.Copy, scale=weights[:, 2:3])
        for r in range(ROW_TILES):
            add_weighted(boths[r], xd[r], 1, parts[r])
        for r in range(ROW_TILES):
            add_weighted(results[r], common[r], 0, boths[r])
            nc.sync.dma_start(out=out[P * r : P * (r + 1), :], in_=results[r][:])
